import numpy as np
import ml_dtypes


def mxq(x, axis, fmt="e4m3"):
    dtype, down = {"e4m3": (ml_dtypes.float8_e4m3fn, 7), "e5m2": (ml_dtypes.float8_e5m2, 14)}[fmt]
    v = np.moveaxis(np.asarray(x, np.float32).astype(ml_dtypes.bfloat16).astype(np.float64), axis, -1)
    blocks = v.reshape(v.shape[:-1] + (-1, 32))
    amax = np.abs(blocks).max(-1, keepdims=True)
    byte = np.maximum(np.where(amax > 0, np.frexp(amax)[1] - 1 + 127, 0) - down, 1)
    scale = np.exp2(byte - 127.0)
    codes = (blocks / scale).astype(np.float32).astype(dtype).astype(np.float64)
    return np.moveaxis((codes * scale).reshape(v.shape), -1, axis)


WIDE = False


def mx_kscale(k):
    if not WIDE:
        return np.ones(k)
    levels = np.array([10, -10, 5, -5, 0])
    a = np.random.permutation(np.resize(levels, k // 512 * 4)).reshape(k // 512, 4)
    idx = np.arange(k)
    return np.exp2(a[idx // 512, idx % 128 // 32])


BF16 = ml_dtypes.bfloat16


def bf(x):
    return np.asarray(x, np.float32).astype(BF16)


def f64(x):
    return np.asarray(x).astype(np.float64)


B, N, C, O = 2, 512, 512, 256
G = 3 * C


def sigmoid(v):
    return 1.0 / (1.0 + np.exp(-v))


def setup_inputs():
    s = mx_kscale(C)
    return {"gx": bf(np.random.standard_normal((B * N, G))),
            "annotations": bf(np.random.standard_normal((B, N, C)) * s),
            "gru_U": bf(np.random.standard_normal((C, G)) / np.sqrt(C) / s[:, None]),
            "gru_b_h": bf(np.random.standard_normal(G) * 0.3),
            "dense_W": bf(np.random.standard_normal((C, O)) * 1.5 / np.sqrt(C) / np.maximum(s, 1.0)[:, None]),
            "dense_b": bf(np.random.standard_normal(O) * 0.1)}


def reference(gx, annotations, gru_U, gru_b_h, dense_W, dense_b):
    h = f64(annotations).reshape(-1, C)
    gh = (mxq(h, 1, "e4m3") @ mxq(f64(gru_U), 0, "e4m3")) + f64(gru_b_h)
    xz, xr, xh = np.split(f64(gx), 3, axis=-1)
    hz, hr, hh = np.split(gh, 3, axis=-1)
    z = sigmoid(xz + hz)
    r = sigmoid(xr + hr)
    hcand = np.tanh(xh + r * hh)
    hnew = z * h + (1.0 - z) * hcand
    out = hnew.reshape(B, N, C)
    return (mxq(out, 2, "e4m3") @ mxq(f64(dense_W), 0, "e4m3")) + f64(dense_b)

@@ -1,0 +1,266 @@
+from contextlib import ExitStack
+
+import concourse.mybir as mybir
+from concourse.masks import make_identity
+
+FP8X4 = mybir.dt.float8_e4m3fn_x4
+BF16 = mybir.dt.bfloat16
+F32 = mybir.dt.float32
+U32 = mybir.dt.uint32
+U8 = mybir.dt.uint8
+ALU = mybir.AluOpType
+ACT = mybir.ActivationFunctionType
+
+P = 128
+LANES = 4
+BLOCKS = 2
+PAIR = 2
+NODES = 1024
+CHANNELS = 512
+GATES = 3
+Z = 0
+R = 1
+CAND = 2
+OUTPUTS = 256
+NODE_TILES = NODES // P
+HALVES = 2
+HALF_TILES = NODE_TILES // HALVES
+HALF = HALF_TILES * P
+SLICE_TILES = 2
+SLICE = SLICE_TILES * P
+
+FLOPS = 2 * NODES * CHANNELS * (GATES * CHANNELS + OUTPUTS)
+
+
+def lane_of_words(words, e):
+    return words.bitcast(BF16).rearrange("p (n e) -> p n e", e=PAIR)[:, :, e]
+
+
+def tile_gatedgraphconvolution_pb_kernel(
+    tc, gx, annotations, gru_U, gru_b_h, dense_W, dense_b, out
+):
+    nc = tc.nc
+    h_rows = annotations.flatten_outer_dims().rearrange("(p a) c -> p a c", a=NODE_TILES)
+    gx_rows = gx.rearrange("(p a) g -> p a g", a=NODE_TILES)
+    out_rows = out.flatten_outer_dims().rearrange("(p a) o -> p a o", a=NODE_TILES)
+
+    with ExitStack() as ctx:
+        const = ctx.enter_context(tc.tile_pool(name="const", bufs=1))
+        inputs = ctx.enter_context(tc.tile_pool(name="inputs", bufs=1))
+        weights = ctx.enter_context(tc.tile_pool(name="weights", bufs=1))
+        halves = ctx.enter_context(tc.tile_pool(name="halves", bufs=1))
+        work = ctx.enter_context(tc.tile_pool(name="work", bufs=2))
+        psum_gh = ctx.enter_context(tc.psum_pool(name="psum_gh", bufs=3))
+        psum_words = ctx.enter_context(tc.psum_pool(name="psum_words", bufs=4))
+        psum_out = ctx.enter_context(tc.psum_pool(name="psum_out", bufs=1))
+
+        h_sb = []
+        gx_sb = []
+        for half in range(HALVES):
+            h_sb.append(inputs.tile([P, HALF_TILES, CHANNELS], BF16, name="h_sb%d" % half))
+            gx_sb.append([])
+            for gate in range(GATES):
+                gx_sb[half].append(
+                    inputs.tile([P, HALF_TILES, CHANNELS], BF16, name="gx_sb%d_%d" % (half, gate))
+                )
+        u_raw = []
+        for gate in range(GATES):
+            u_raw.append(weights.tile([P, LANES, CHANNELS], BF16, name="u_raw%d" % gate))
+        w_raw = weights.tile([P, LANES, OUTPUTS], BF16)
+
+        def load_lanes(raw, rows):
+            for u in range(BLOCKS):
+                nc.sync.dma_start(
+                    out=raw[:, PAIR * u : PAIR * (u + 1), :],
+                    in_=rows[PAIR * P * u : PAIR * P * (u + 1), :].rearrange(
+                        "(q e) w -> q e w", e=PAIR
+                    ),
+                )
+
+        for half in range(HALVES):
+            tiles = slice(half * HALF_TILES, (half + 1) * HALF_TILES)
+            nc.sync.dma_start(out=h_sb[half][:], in_=h_rows[:, tiles, :])
+            for gate in range(GATES):
+                cols = slice(gate * CHANNELS, (gate + 1) * CHANNELS)
+                if half == 0:
+                    load_lanes(u_raw[gate], gru_U[:, cols])
+                nc.sync.dma_start(out=gx_sb[half][gate][:], in_=gx_rows[:, tiles, cols])
+            if half == 0:
+                load_lanes(w_raw, dense_W)
+
+        ident = const.tile([P, P], F32)
+        make_identity(nc, ident[:])
+
+        warm = const.tile([P, 1], F32)
+        nc.vector.memset(warm[:], 0.0)
+        nc.scalar.activation(out=warm[:], in_=warm[:], func=ACT.Sigmoid)
+
+        bias_rows = const.tile([P, PAIR * P], BF16)
+        nc.vector.memset(bias_rows[:], 0.0)
+        nc.scalar.dma_start(
+            out=bias_rows[0 : GATES * BLOCKS, :],
+            in_=gru_b_h.rearrange("(r c) -> r c", c=PAIR * P),
+        )
+        bias_bank = psum_words.tile([P, HALF], F32, tag="words")
+        nc.tensor.transpose(bias_bank[:, 0:P], bias_rows[:].bitcast(F32), ident[:])
+        gate_bias = const.tile([P, GATES * LANES], F32)
+        nc.vector.tensor_copy(out=gate_bias[:], in_=bias_bank[:, 0 : GATES * BLOCKS].bitcast(BF16))
+
+        dense_bias = const.tile([P, OUTPUTS], BF16)
+        nc.scalar.dma_start(out=dense_bias[:], in_=dense_b.partition_broadcast(P))
+
+        u_codes = []
+        u_scales = []
+        for gate in range(GATES):
+            u_grouped = weights.tile(
+                [P, CHANNELS, LANES], BF16, name="u_grouped%d" % gate, align_bytes=64
+            )
+            copy = nc.vector.tensor_copy if gate == Z else nc.scalar.copy
+            for u in range(BLOCKS):
+                block = slice(PAIR * P * u, PAIR * P * (u + 1))
+                copy(
+                    out=u_grouped[:, block, :].rearrange("k (e q) t -> k e q t", e=PAIR),
+                    in_=u_raw[gate][:, :, block].rearrange("k t (q e) -> k e q t", e=PAIR),
+                )
+            u_codes.append(weights.tile([P, CHANNELS], U32, name="u_codes%d" % gate, align_bytes=64))
+            u_scales.append(weights.tile([P, CHANNELS], U8, name="u_scales%d" % gate, align_bytes=64))
+            nc.vector.quantize_mx(
+                out=u_codes[gate][:].bitcast(FP8X4),
+                scales=u_scales[gate][:],
+                in_=u_grouped[:].rearrange("k w t -> k (w t)"),
+            )
+
+        w_grouped = weights.tile([P, OUTPUTS, LANES], BF16, align_bytes=64)
+        nc.scalar.copy(out=w_grouped[:], in_=w_raw[:].rearrange("k t w -> k w t"))
+        w_codes = weights.tile([P, OUTPUTS], U32, align_bytes=64)
+        w_scales = weights.tile([P, OUTPUTS], U8, align_bytes=64)
+        nc.vector.quantize_mx(
+            out=w_codes[:].bitcast(FP8X4),
+            scales=w_scales[:],
+            in_=w_grouped[:].rearrange("k w t -> k (w t)"),
+        )
+
+        def transposed_gx(half, gate, u):
+            bank = psum_words.tile([P, HALF], F32, tag="words")
+            for a in range(HALF_TILES):
+                nc.tensor.transpose(
+                    bank[:, a * P : (a + 1) * P],
+                    gx_sb[half][gate][:, a, :].bitcast(F32)[:, u * P : (u + 1) * P],
+                    ident[:],
+                )
+            return bank
+
+        def gh_bank(h_codes, h_scales, gate, t):
+            bank = psum_gh.tile([P, HALF], F32, tag="gh")
+            positions = slice(t * P, (t + 1) * P)
+            nc.tensor.matmul_mx(
+                out=bank[:],
+                lhsT=u_codes[gate][:, positions].bitcast(FP8X4),
+                lhsT_scale=u_scales[gate][:, positions],
+                rhs=h_codes[:].bitcast(FP8X4),
+                rhs_scale=h_scales[:],
+                start=True,
+                stop=True,
+            )
+            return bank
+
+        for half in range(HALVES):
+            h_words = halves.tile([P, HALF, BLOCKS], F32, name="h_words%d" % half, align_bytes=64)
+            for s in range(HALF_TILES // SLICE_TILES):
+                bank = psum_words.tile([P, BLOCKS, SLICE], F32, tag="words")
+                for u in range(BLOCKS):
+                    for j in range(SLICE_TILES):
+                        nc.tensor.transpose(
+                            bank[:, u, j * P : (j + 1) * P],
+                            h_sb[half][:, s * SLICE_TILES + j, :].bitcast(F32)[:, u * P : (u + 1) * P],
+                            ident[:],
+                        )
+                nc.scalar.copy(
+                    out=h_words[:, s * SLICE : (s + 1) * SLICE, :],
+                    in_=bank[:].rearrange("q u n -> q n u"),
+                )
+            h_lanes = h_words[:].rearrange("q n u -> q (n u)").bitcast(BF16)
+            h_codes = halves.tile([P, HALF], U32, name="h_codes%d" % half, align_bytes=64)
+            h_scales = halves.tile([P, HALF], U8, name="h_scales%d" % half, align_bytes=64)
+            nc.vector.quantize_mx(out=h_codes[:].bitcast(FP8X4), scales=h_scales[:], in_=h_lanes)
+
+            sigmoids = []
+            for gate in (Z, R):
+                x_words = halves.tile([P, BLOCKS, HALF], F32, name="x_words%d_%d" % (half, gate))
+                for u in range(BLOCKS):
+                    nc.scalar.copy(out=x_words[:, u, :], in_=transposed_gx(half, gate, u)[:])
+                sigmoid = halves.tile([P, LANES, HALF], F32, name="sigmoid%d_%d" % (half, gate))
+                for t in range(LANES):
+                    nc.vector.scalar_tensor_tensor(
+                        out=sigmoid[:, t, :],
+                        in0=gh_bank(h_codes, h_scales, gate, t)[:],
+                        scalar=gate_bias[:, gate * LANES + t : gate * LANES + t + 1],
+                        in1=lane_of_words(x_words[:, t // PAIR, :], t % PAIR),
+                        op0=ALU.add,
+                        op1=ALU.add,
+                    )
+                    nc.scalar.activation(out=sigmoid[:, t, :], in_=sigmoid[:, t, :], func=ACT.Sigmoid)
+                sigmoids.append(sigmoid)
+            z, r = sigmoids
+
+            cand = halves.tile([P, LANES, HALF], F32, name="cand%d" % half)
+            for t in range(LANES):
+                nc.vector.scalar_tensor_tensor(
+                    out=cand[:, t, :],
+                    in0=gh_bank(h_codes, h_scales, CAND, t)[:],
+                    scalar=gate_bias[:, CAND * LANES + t : CAND * LANES + t + 1],
+                    in1=r[:, t, :],
+                    op0=ALU.add,
+                    op1=ALU.mult,
+                )
+            for u in range(BLOCKS):
+                x_bank = transposed_gx(half, CAND, u)
+                for e in range(PAIR):
+                    t = PAIR * u + e
+                    nc.vector.tensor_tensor(
+                        out=cand[:, t, :], in0=cand[:, t, :], in1=lane_of_words(x_bank[:], e), op=ALU.add
+                    )
+                    nc.scalar.activation(out=cand[:, t, :], in_=cand[:, t, :], func=ACT.Tanh)
+
+            h_by_lane = h_lanes.rearrange("q (n t) -> q t n", t=LANES)
+            for s in range(HALF_TILES // SLICE_TILES):
+                nodes = slice(s * SLICE, (s + 1) * SLICE)
+                mix = work.tile([P, LANES, SLICE], F32)
+                nc.vector.tensor_tensor(
+                    out=mix[:], in0=h_by_lane[:, :, nodes], in1=cand[:, :, nodes], op=ALU.subtract
+                )
+                nc.vector.tensor_tensor(out=mix[:], in0=mix[:], in1=z[:, :, nodes], op=ALU.mult)
+                hnew = work.tile([P, LANES, SLICE], BF16)
+                nc.vector.tensor_tensor(out=hnew[:], in0=mix[:], in1=cand[:, :, nodes], op=ALU.add)
+                hnew_grouped = work.tile([P, SLICE, LANES], BF16, align_bytes=64)
+                nc.scalar.copy(out=hnew_grouped[:], in_=hnew[:].rearrange("q t n -> q n t"))
+                hnew_codes = work.tile([P, SLICE], U32, align_bytes=64)
+                hnew_scales = work.tile([P, SLICE], U8, align_bytes=64)
+                nc.vector.quantize_mx(
+                    out=hnew_codes[:].bitcast(FP8X4),
+                    scales=hnew_scales[:],
+                    in_=hnew_grouped[:].rearrange("q n t -> q (n t)"),
+                )
+                out_bank = psum_out.tile([P, SLICE_TILES, OUTPUTS], F32)
+                for j in range(SLICE_TILES):
+                    tile_nodes = slice(j * P, (j + 1) * P)
+                    nc.tensor.matmul_mx(
+                        out=out_bank[:, j, :],
+                        lhsT=hnew_codes[:, tile_nodes].bitcast(FP8X4),
+                        lhsT_scale=hnew_scales[:, tile_nodes],
+                        rhs=w_codes[:].bitcast(FP8X4),
+                        rhs_scale=w_scales[:],
+                        start=True,
+                        stop=True,
+                    )
+                out_sb = work.tile([P, SLICE_TILES, OUTPUTS], F32)
+                nc.vector.tensor_tensor(
+                    out=out_sb[:],
+                    in0=out_bank[:],
+                    in1=dense_bias[:].unsqueeze(1).to_broadcast([P, SLICE_TILES, OUTPUTS]),
+                    op=ALU.add,
+                )
+                first_tile = half * HALF_TILES + s * SLICE_TILES
+                nc.sync.dma_start(
+                    out=out_rows[:, first_tile : first_tile + SLICE_TILES, :], in_=out_sb[:]
+                )

@@ -51,8 +51,8 @@ def tile_gatedgraphconvolution_pb_kernel(
         halves = ctx.enter_context(tc.tile_pool(name="halves", bufs=1))
         work = ctx.enter_context(tc.tile_pool(name="work", bufs=2))
         psum_gh = ctx.enter_context(tc.psum_pool(name="psum_gh", bufs=3))
-        psum_words = ctx.enter_context(tc.psum_pool(name="psum_words", bufs=4))
-        psum_out = ctx.enter_context(tc.psum_pool(name="psum_out", bufs=1))
+        psum_words = ctx.enter_context(tc.psum_pool(name="psum_words", bufs=3))
+        psum_out = ctx.enter_context(tc.psum_pool(name="psum_out", bufs=2))
 
         h_sb = []
         gx_sb = []
@@ -67,26 +67,47 @@ def tile_gatedgraphconvolution_pb_kernel(
         for gate in range(GATES):
             u_raw.append(weights.tile([P, LANES, CHANNELS], BF16, name="u_raw%d" % gate))
         w_raw = weights.tile([P, LANES, OUTPUTS], BF16)
+        bias_rows = const.tile([P, PAIR * P], BF16)
+        dense_bias = const.tile([P, OUTPUTS], BF16)
 
-        def load_lanes(raw, rows):
+        def load_lanes(queue, raw, rows):
             for u in range(BLOCKS):
-                nc.sync.dma_start(
+                queue.dma_start(
                     out=raw[:, PAIR * u : PAIR * (u + 1), :],
                     in_=rows[PAIR * P * u : PAIR * P * (u + 1), :].rearrange(
                         "(q e) w -> q e w", e=PAIR
                     ),
                 )
 
-        for half in range(HALVES):
+        def load_u(gate):
+            load_lanes(nc.sync, u_raw[gate], gru_U[:, gate * CHANNELS : (gate + 1) * CHANNELS])
+
+        def load_h(half):
             tiles = slice(half * HALF_TILES, (half + 1) * HALF_TILES)
             nc.sync.dma_start(out=h_sb[half][:], in_=h_rows[:, tiles, :])
-            for gate in range(GATES):
-                cols = slice(gate * CHANNELS, (gate + 1) * CHANNELS)
-                if half == 0:
-                    load_lanes(u_raw[gate], gru_U[:, cols])
-                nc.sync.dma_start(out=gx_sb[half][gate][:], in_=gx_rows[:, tiles, cols])
-            if half == 0:
-                load_lanes(w_raw, dense_W)
+
+        def load_gx(half, gate):
+            tiles = slice(half * HALF_TILES, (half + 1) * HALF_TILES)
+            cols = slice(gate * CHANNELS, (gate + 1) * CHANNELS)
+            nc.sync.dma_start(out=gx_sb[half][gate][:], in_=gx_rows[:, tiles, cols])
+
+        nc.vector.memset(bias_rows[:], 0.0)
+        nc.scalar.dma_start(
+            out=bias_rows[0 : GATES * BLOCKS, :],
+            in_=gru_b_h.rearrange("(r c) -> r c", c=PAIR * P),
+        )
+        load_lanes(nc.scalar, w_raw, dense_W)
+        load_u(Z)
+        load_h(0)
+        load_gx(0, Z)
+        load_u(R)
+        load_gx(0, R)
+        load_gx(0, CAND)
+        load_u(CAND)
+        load_h(1)
+        for gate in range(GATES):
+            load_gx(1, gate)
+        nc.sync.dma_start(out=dense_bias[:], in_=dense_b.partition_broadcast(P))
 
         ident = const.tile([P, P], F32)
         make_identity(nc, ident[:])
@@ -95,50 +116,27 @@ def tile_gatedgraphconvolution_pb_kernel(
         nc.vector.memset(warm[:], 0.0)
         nc.scalar.activation(out=warm[:], in_=warm[:], func=ACT.Sigmoid)
 
-        bias_rows = const.tile([P, PAIR * P], BF16)
-        nc.vector.memset(bias_rows[:], 0.0)
-        nc.scalar.dma_start(
-            out=bias_rows[0 : GATES * BLOCKS, :],
-            in_=gru_b_h.rearrange("(r c) -> r c", c=PAIR * P),
-        )
-        bias_bank = psum_words.tile([P, HALF], F32, tag="words")
-        nc.tensor.transpose(bias_bank[:, 0:P], bias_rows[:].bitcast(F32), ident[:])
-        gate_bias = const.tile([P, GATES * LANES], F32)
-        nc.vector.tensor_copy(out=gate_bias[:], in_=bias_bank[:, 0 : GATES * BLOCKS].bitcast(BF16))
-
-        dense_bias = const.tile([P, OUTPUTS], BF16)
-        nc.scalar.dma_start(out=dense_bias[:], in_=dense_b.partition_broadcast(P))
-
         u_codes = []
         u_scales = []
         for gate in range(GATES):
+            u_codes.append(weights.tile([P, CHANNELS], U32, name="u_codes%d" % gate, align_bytes=64))
+            u_scales.append(weights.tile([P, CHANNELS], U8, name="u_scales%d" % gate, align_bytes=64))
+
+        def quantise_u(gate):
             u_grouped = weights.tile(
                 [P, CHANNELS, LANES], BF16, name="u_grouped%d" % gate, align_bytes=64
             )
-            copy = nc.vector.tensor_copy if gate == Z else nc.scalar.copy
             for u in range(BLOCKS):
                 block = slice(PAIR * P * u, PAIR * P * (u + 1))
-                copy(
+                nc.vector.tensor_copy(
                     out=u_grouped[:, block, :].rearrange("k (e q) t -> k e q t", e=PAIR),
                     in_=u_raw[gate][:, :, block].rearrange("k t (q e) -> k e q t", e=PAIR),
                 )
-            u_codes.append(weights.tile([P, CHANNELS], U32, name="u_codes%d" % gate, align_bytes=64))
-            u_scales.append(weights.tile([P, CHANNELS], U8, name="u_scales%d" % gate, align_bytes=64))
             nc.vector.quantize_mx(
                 out=u_codes[gate][:].bitcast(FP8X4),
                 scales=u_scales[gate][:],
                 in_=u_grouped[:].rearrange("k w t -> k (w t)"),
             )
-
-        w_grouped = weights.tile([P, OUTPUTS, LANES], BF16, align_bytes=64)
-        nc.scalar.copy(out=w_grouped[:], in_=w_raw[:].rearrange("k t w -> k w t"))
-        w_codes = weights.tile([P, OUTPUTS], U32, align_bytes=64)
-        w_scales = weights.tile([P, OUTPUTS], U8, align_bytes=64)
-        nc.vector.quantize_mx(
-            out=w_codes[:].bitcast(FP8X4),
-            scales=w_scales[:],
-            in_=w_grouped[:].rearrange("k w t -> k (w t)"),
-        )
 
         def transposed_gx(half, gate, u):
             bank = psum_words.tile([P, HALF], F32, tag="words")
@@ -150,21 +148,13 @@ def tile_gatedgraphconvolution_pb_kernel(
                 )
             return bank
 
-        def gh_bank(h_codes, h_scales, gate, t):
-            bank = psum_gh.tile([P, HALF], F32, tag="gh")
-            positions = slice(t * P, (t + 1) * P)
-            nc.tensor.matmul_mx(
-                out=bank[:],
-                lhsT=u_codes[gate][:, positions].bitcast(FP8X4),
-                lhsT_scale=u_scales[gate][:, positions],
-                rhs=h_codes[:].bitcast(FP8X4),
-                rhs_scale=h_scales[:],
-                start=True,
-                stop=True,
-            )
-            return bank
+        def gx_words_in_sbuf(half, gate):
+            x_words = halves.tile([P, BLOCKS, HALF], F32, name="x_words%d_%d" % (half, gate))
+            for u in range(BLOCKS):
+                nc.scalar.copy(out=x_words[:, u, :], in_=transposed_gx(half, gate, u)[:])
+            return x_words
 
-        for half in range(HALVES):
+        def transposed_h(half):
             h_words = halves.tile([P, HALF, BLOCKS], F32, name="h_words%d" % half, align_bytes=64)
             for s in range(HALF_TILES // SLICE_TILES):
                 bank = psum_words.tile([P, BLOCKS, SLICE], F32, tag="words")
@@ -179,67 +169,111 @@ def tile_gatedgraphconvolution_pb_kernel(
                     out=h_words[:, s * SLICE : (s + 1) * SLICE, :],
                     in_=bank[:].rearrange("q u n -> q n u"),
                 )
-            h_lanes = h_words[:].rearrange("q n u -> q (n u)").bitcast(BF16)
+            return h_words[:].rearrange("q n u -> q (n u)").bitcast(BF16)
+
+        def quantise_h(half, h_lanes):
             h_codes = halves.tile([P, HALF], U32, name="h_codes%d" % half, align_bytes=64)
             h_scales = halves.tile([P, HALF], U8, name="h_scales%d" % half, align_bytes=64)
             nc.vector.quantize_mx(out=h_codes[:].bitcast(FP8X4), scales=h_scales[:], in_=h_lanes)
+            return h_codes, h_scales
 
-            sigmoids = []
-            for gate in (Z, R):
-                x_words = halves.tile([P, BLOCKS, HALF], F32, name="x_words%d_%d" % (half, gate))
-                for u in range(BLOCKS):
-                    nc.scalar.copy(out=x_words[:, u, :], in_=transposed_gx(half, gate, u)[:])
-                sigmoid = halves.tile([P, LANES, HALF], F32, name="sigmoid%d_%d" % (half, gate))
-                for t in range(LANES):
-                    nc.vector.scalar_tensor_tensor(
-                        out=sigmoid[:, t, :],
-                        in0=gh_bank(h_codes, h_scales, gate, t)[:],
-                        scalar=gate_bias[:, gate * LANES + t : gate * LANES + t + 1],
-                        in1=lane_of_words(x_words[:, t // PAIR, :], t % PAIR),
-                        op0=ALU.add,
-                        op1=ALU.add,
-                    )
-                    nc.scalar.activation(out=sigmoid[:, t, :], in_=sigmoid[:, t, :], func=ACT.Sigmoid)
-                sigmoids.append(sigmoid)
-            z, r = sigmoids
+        def gh_bank(h_mx, gate, t):
+            h_codes, h_scales = h_mx
+            bank = psum_gh.tile([P, HALF], F32, tag="gh")
+            positions = slice(t * P, (t + 1) * P)
+            nc.tensor.matmul_mx(
+                out=bank[:],
+                lhsT=u_codes[gate][:, positions].bitcast(FP8X4),
+                lhsT_scale=u_scales[gate][:, positions],
+                rhs=h_codes[:].bitcast(FP8X4),
+                rhs_scale=h_scales[:],
+                start=True,
+                stop=True,
+            )
+            return bank
 
+        def sigmoid_gate(half, gate, h_mx, x_words):
+            sigmoid = halves.tile([P, LANES, HALF], F32, name="sigmoid%d_%d" % (half, gate))
+            for t in range(LANES):
+                nc.vector.scalar_tensor_tensor(
+                    out=sigmoid[:, t, :],
+                    in0=gh_bank(h_mx, gate, t)[:],
+                    scalar=gate_bias[:, gate * LANES + t : gate * LANES + t + 1],
+                    in1=lane_of_words(x_words[:, t // PAIR, :], t % PAIR),
+                    op0=ALU.add,
+                    op1=ALU.add,
+                )
+                nc.scalar.activation(out=sigmoid[:, t, :], in_=sigmoid[:, t, :], func=ACT.Sigmoid)
+            return sigmoid
+
+        def candidate(half, h_mx, x_banks, r):
             cand = halves.tile([P, LANES, HALF], F32, name="cand%d" % half)
             for t in range(LANES):
                 nc.vector.scalar_tensor_tensor(
                     out=cand[:, t, :],
-                    in0=gh_bank(h_codes, h_scales, CAND, t)[:],
+                    in0=gh_bank(h_mx, CAND, t)[:],
                     scalar=gate_bias[:, CAND * LANES + t : CAND * LANES + t + 1],
                     in1=r[:, t, :],
                     op0=ALU.add,
                     op1=ALU.mult,
                 )
-            for u in range(BLOCKS):
-                x_bank = transposed_gx(half, CAND, u)
-                for e in range(PAIR):
-                    t = PAIR * u + e
-                    nc.vector.tensor_tensor(
-                        out=cand[:, t, :], in0=cand[:, t, :], in1=lane_of_words(x_bank[:], e), op=ALU.add
-                    )
-                    nc.scalar.activation(out=cand[:, t, :], in_=cand[:, t, :], func=ACT.Tanh)
-
-            h_by_lane = h_lanes.rearrange("q (n t) -> q t n", t=LANES)
-            for s in range(HALF_TILES // SLICE_TILES):
-                nodes = slice(s * SLICE, (s + 1) * SLICE)
-                mix = work.tile([P, LANES, SLICE], F32)
+            for t in range(LANES):
                 nc.vector.tensor_tensor(
-                    out=mix[:], in0=h_by_lane[:, :, nodes], in1=cand[:, :, nodes], op=ALU.subtract
+                    out=cand[:, t, :],
+                    in0=cand[:, t, :],
+                    in1=lane_of_words(x_banks[t // PAIR][:], t % PAIR),
+                    op=ALU.add,
                 )
-                nc.vector.tensor_tensor(out=mix[:], in0=mix[:], in1=z[:, :, nodes], op=ALU.mult)
-                hnew = work.tile([P, LANES, SLICE], BF16)
-                nc.vector.tensor_tensor(out=hnew[:], in0=mix[:], in1=cand[:, :, nodes], op=ALU.add)
-                hnew_grouped = work.tile([P, SLICE, LANES], BF16, align_bytes=64)
-                nc.scalar.copy(out=hnew_grouped[:], in_=hnew[:].rearrange("q t n -> q n t"))
+                nc.scalar.activation(out=cand[:, t, :], in_=cand[:, t, :], func=ACT.Tanh)
+            return cand
+
+        def kept_state(half, z, h_lanes):
+            kept = halves.tile([P, LANES, HALF], F32, name="kept%d" % half)
+            h_by_lane = h_lanes.rearrange("q (n t) -> q t n", t=LANES)
+            for u in range(BLOCKS):
+                lanes = slice(PAIR * u, PAIR * (u + 1))
+                nc.gpsimd.tensor_tensor(
+                    out=kept[:, lanes, :], in0=z[:, lanes, :], in1=h_by_lane[:, lanes, :], op=ALU.mult
+                )
+            return kept
+
+        def new_state(half, z, kept, cand):
+            hnew = halves.tile([P, LANES, HALF], BF16, name="hnew%d" % half)
+            for u in range(BLOCKS):
+                lanes = slice(PAIR * u, PAIR * (u + 1))
+                minus_new = work.tile([P, PAIR, HALF], F32)
+                nc.vector.scalar_tensor_tensor(
+                    out=minus_new[:],
+                    in0=z[:, lanes, :],
+                    scalar=1.0,
+                    in1=cand[:, lanes, :],
+                    op0=ALU.subtract,
+                    op1=ALU.mult,
+                )
+                nc.vector.tensor_tensor(
+                    out=hnew[:, lanes, :], in0=kept[:, lanes, :], in1=minus_new[:], op=ALU.subtract
+                )
+            grouped = []
+            for s in range(HALF_TILES // SLICE_TILES):
+                hnew_grouped = halves.tile(
+                    [P, SLICE, LANES], BF16, name="hnew_grouped%d_%d" % (half, s), align_bytes=64
+                )
+                nc.scalar.copy(
+                    out=hnew_grouped[:],
+                    in_=hnew[:, :, s * SLICE : (s + 1) * SLICE].rearrange("q t n -> q n t"),
+                )
+                grouped.append(hnew_grouped)
+            return grouped
+
+        def readout(half, grouped):
+            out_banks = []
+            for s in range(HALF_TILES // SLICE_TILES):
                 hnew_codes = work.tile([P, SLICE], U32, align_bytes=64)
                 hnew_scales = work.tile([P, SLICE], U8, align_bytes=64)
                 nc.vector.quantize_mx(
                     out=hnew_codes[:].bitcast(FP8X4),
                     scales=hnew_scales[:],
-                    in_=hnew_grouped[:].rearrange("q n t -> q (n t)"),
+                    in_=grouped[s][:].rearrange("q n t -> q (n t)"),
                 )
                 out_bank = psum_out.tile([P, SLICE_TILES, OUTPUTS], F32)
                 for j in range(SLICE_TILES):
@@ -253,10 +287,12 @@ def tile_gatedgraphconvolution_pb_kernel(
                         start=True,
                         stop=True,
                     )
+                out_banks.append(out_bank)
+            for s in range(HALF_TILES // SLICE_TILES):
                 out_sb = work.tile([P, SLICE_TILES, OUTPUTS], F32)
                 nc.vector.tensor_tensor(
                     out=out_sb[:],
-                    in0=out_bank[:],
+                    in0=out_banks[s][:],
                     in1=dense_bias[:].unsqueeze(1).to_broadcast([P, SLICE_TILES, OUTPUTS]),
                     op=ALU.add,
                 )
@@ -264,3 +300,46 @@ def tile_gatedgraphconvolution_pb_kernel(
                 nc.sync.dma_start(
                     out=out_rows[:, first_tile : first_tile + SLICE_TILES, :], in_=out_sb[:]
                 )
+
+        quantise_u(Z)
+        h_lanes = transposed_h(0)
+        x_words_z = gx_words_in_sbuf(0, Z)
+        h_mx = quantise_h(0, h_lanes)
+
+        bias_bank = psum_words.tile([P, HALF], F32, tag="words")
+        nc.tensor.transpose(bias_bank[:, 0:P], bias_rows[:].bitcast(F32), ident[:])
+        gate_bias = const.tile([P, GATES * LANES], F32)
+        nc.vector.tensor_copy(out=gate_bias[:], in_=bias_bank[:, 0 : GATES * BLOCKS].bitcast(BF16))
+
+        quantise_u(R)
+
+        w_grouped = weights.tile([P, OUTPUTS, LANES], BF16, align_bytes=64)
+        nc.scalar.copy(out=w_grouped[:], in_=w_raw[:].rearrange("k t w -> k w t"))
+        w_codes = weights.tile([P, OUTPUTS], U32, align_bytes=64)
+        w_scales = weights.tile([P, OUTPUTS], U8, align_bytes=64)
+        nc.vector.quantize_mx(
+            out=w_codes[:].bitcast(FP8X4),
+            scales=w_scales[:],
+            in_=w_grouped[:].rearrange("k w t -> k (w t)"),
+        )
+
+        for half in range(HALVES):
+            z = sigmoid_gate(half, Z, h_mx, x_words_z)
+            kept = kept_state(half, z, h_lanes)
+            x_words_r = gx_words_in_sbuf(half, R)
+            x_banks = []
+            for u in range(BLOCKS):
+                x_banks.append(transposed_gx(half, CAND, u))
+            if half == 0:
+                quantise_u(CAND)
+            else:
+                readout(half - 1, grouped)
+            r = sigmoid_gate(half, R, h_mx, x_words_r)
+            cand = candidate(half, h_mx, x_banks, r)
+            if half + 1 < HALVES:
+                h_lanes = transposed_h(half + 1)
+                x_words_z = gx_words_in_sbuf(half + 1, Z)
+            grouped = new_state(half, z, kept, cand)
+            if half + 1 < HALVES:
+                h_mx = quantise_h(half + 1, h_lanes)
+        readout(HALVES - 1, grouped)

@@ -53,6 +53,7 @@ def tile_gatedgraphconvolution_pb_kernel(
         psum_gh = ctx.enter_context(tc.psum_pool(name="psum_gh", bufs=3))
         psum_words = ctx.enter_context(tc.psum_pool(name="psum_words", bufs=3))
         psum_out = ctx.enter_context(tc.psum_pool(name="psum_out", bufs=2))
+        ctx.enter_context(tc.manual_schedule())
 
         h_sb = []
         gx_sb = []

@@ -50,9 +50,10 @@ def tile_gatedgraphconvolution_pb_kernel(
         weights = ctx.enter_context(tc.tile_pool(name="weights", bufs=1))
         halves = ctx.enter_context(tc.tile_pool(name="halves", bufs=1))
         work = ctx.enter_context(tc.tile_pool(name="work", bufs=2))
+        results = ctx.enter_context(tc.tile_pool(name="results", bufs=4))
         psum_gh = ctx.enter_context(tc.psum_pool(name="psum_gh", bufs=3))
         psum_words = ctx.enter_context(tc.psum_pool(name="psum_words", bufs=3))
-        psum_out = ctx.enter_context(tc.psum_pool(name="psum_out", bufs=2))
+        psum_pairs = ctx.enter_context(tc.psum_pool(name="psum_pairs", bufs=2))
         ctx.enter_context(tc.manual_schedule())
 
         h_sb = []
@@ -98,13 +99,13 @@ def tile_gatedgraphconvolution_pb_kernel(
             in_=gru_b_h.rearrange("(r c) -> r c", c=PAIR * P),
         )
         load_lanes(nc.scalar, w_raw, dense_W)
-        load_u(Z)
         load_h(0)
-        load_gx(0, Z)
+        load_u(Z)
         load_u(R)
+        load_gx(0, Z)
+        load_u(CAND)
         load_gx(0, R)
         load_gx(0, CAND)
-        load_u(CAND)
         load_h(1)
         for gate in range(GATES):
             load_gx(1, gate)
@@ -123,16 +124,28 @@ def tile_gatedgraphconvolution_pb_kernel(
             u_codes.append(weights.tile([P, CHANNELS], U32, name="u_codes%d" % gate, align_bytes=64))
             u_scales.append(weights.tile([P, CHANNELS], U8, name="u_scales%d" % gate, align_bytes=64))
 
-        def quantise_u(gate):
+        def group_u(gate, on_gpsimd):
             u_grouped = weights.tile(
                 [P, CHANNELS, LANES], BF16, name="u_grouped%d" % gate, align_bytes=64
             )
             for u in range(BLOCKS):
                 block = slice(PAIR * P * u, PAIR * P * (u + 1))
-                nc.vector.tensor_copy(
-                    out=u_grouped[:, block, :].rearrange("k (e q) t -> k e q t", e=PAIR),
-                    in_=u_raw[gate][:, :, block].rearrange("k t (q e) -> k e q t", e=PAIR),
-                )
+                sorted_columns = u_grouped[:, block, :].rearrange("k (e q) t -> k e q t", e=PAIR)
+                columns = u_raw[gate][:, :, block].rearrange("k t (q e) -> k e q t", e=PAIR)
+                if on_gpsimd:
+                    nc.gpsimd.tensor_scalar(
+                        out=sorted_columns,
+                        in0=columns,
+                        scalar1=1.0,
+                        scalar2=0.0,
+                        op0=ALU.mult,
+                        op1=ALU.add,
+                    )
+                else:
+                    nc.vector.tensor_copy(out=sorted_columns, in_=columns)
+            return u_grouped
+
+        def quantise_u(gate, u_grouped):
             nc.vector.quantize_mx(
                 out=u_codes[gate][:].bitcast(FP8X4),
                 scales=u_scales[gate][:],
@@ -158,7 +171,7 @@ def tile_gatedgraphconvolution_pb_kernel(
         def transposed_h(half):
             h_words = halves.tile([P, HALF, BLOCKS], F32, name="h_words%d" % half, align_bytes=64)
             for s in range(HALF_TILES // SLICE_TILES):
-                bank = psum_words.tile([P, BLOCKS, SLICE], F32, tag="words")
+                bank = psum_pairs.tile([P, BLOCKS, SLICE], F32, tag="pair")
                 for u in range(BLOCKS):
                     for j in range(SLICE_TILES):
                         nc.tensor.transpose(
@@ -193,23 +206,25 @@ def tile_gatedgraphconvolution_pb_kernel(
             )
             return bank
 
-        def sigmoid_gate(half, gate, h_mx, x_words):
-            sigmoid = halves.tile([P, LANES, HALF], F32, name="sigmoid%d_%d" % (half, gate))
+        def gate_sums(half, gate, h_mx, x_words):
+            sums = halves.tile([P, LANES, HALF], F32, name="gate%d_%d" % (half, gate))
             for t in range(LANES):
                 nc.vector.scalar_tensor_tensor(
-                    out=sigmoid[:, t, :],
+                    out=sums[:, t, :],
                     in0=gh_bank(h_mx, gate, t)[:],
                     scalar=gate_bias[:, gate * LANES + t : gate * LANES + t + 1],
                     in1=lane_of_words(x_words[:, t // PAIR, :], t % PAIR),
                     op0=ALU.add,
                     op1=ALU.add,
                 )
-                nc.scalar.activation(out=sigmoid[:, t, :], in_=sigmoid[:, t, :], func=ACT.Sigmoid)
-            return sigmoid
+            return sums
 
-        def candidate(half, h_mx, x_banks, r):
-            cand = halves.tile([P, LANES, HALF], F32, name="cand%d" % half)
+        def sigmoid_in_place(sums):
             for t in range(LANES):
+                nc.scalar.activation(out=sums[:, t, :], in_=sums[:, t, :], func=ACT.Sigmoid)
+
+        def candidate_block(cand, u, h_mx, x_bank, r):
+            for t in range(PAIR * u, PAIR * (u + 1)):
                 nc.vector.scalar_tensor_tensor(
                     out=cand[:, t, :],
                     in0=gh_bank(h_mx, CAND, t)[:],
@@ -218,17 +233,25 @@ def tile_gatedgraphconvolution_pb_kernel(
                     op0=ALU.add,
                     op1=ALU.mult,
                 )
-            for t in range(LANES):
+            for t in range(PAIR * u, PAIR * (u + 1)):
                 nc.vector.tensor_tensor(
                     out=cand[:, t, :],
                     in0=cand[:, t, :],
-                    in1=lane_of_words(x_banks[t // PAIR][:], t % PAIR),
+                    in1=lane_of_words(x_bank[:], t % PAIR),
                     op=ALU.add,
                 )
                 nc.scalar.activation(out=cand[:, t, :], in_=cand[:, t, :], func=ACT.Tanh)
-            return cand
 
         def kept_state(half, z, h_lanes):
+            z_minus_1 = halves.tile([P, PAIR, HALF], F32, name="z_minus_1_%d" % half)
+            nc.gpsimd.tensor_scalar(
+                out=z_minus_1[:],
+                in0=z[:, 0:PAIR, :],
+                scalar1=1.0,
+                scalar2=-1.0,
+                op0=ALU.mult,
+                op1=ALU.add,
+            )
             kept = halves.tile([P, LANES, HALF], F32, name="kept%d" % half)
             h_by_lane = h_lanes.rearrange("q (n t) -> q t n", t=LANES)
             for u in range(BLOCKS):
@@ -236,111 +259,147 @@ def tile_gatedgraphconvolution_pb_kernel(
                 nc.gpsimd.tensor_tensor(
                     out=kept[:, lanes, :], in0=z[:, lanes, :], in1=h_by_lane[:, lanes, :], op=ALU.mult
                 )
-            return kept
+            return z_minus_1, kept
 
-        def new_state(half, z, kept, cand):
-            hnew = halves.tile([P, LANES, HALF], BF16, name="hnew%d" % half)
-            for u in range(BLOCKS):
-                lanes = slice(PAIR * u, PAIR * (u + 1))
-                minus_new = work.tile([P, PAIR, HALF], F32)
-                nc.vector.scalar_tensor_tensor(
-                    out=minus_new[:],
-                    in0=z[:, lanes, :],
-                    scalar=1.0,
-                    in1=cand[:, lanes, :],
-                    op0=ALU.subtract,
-                    op1=ALU.mult,
-                )
-                nc.vector.tensor_tensor(
-                    out=hnew[:, lanes, :], in0=kept[:, lanes, :], in1=minus_new[:], op=ALU.subtract
-                )
+        def group_new_state(half, hnew):
             grouped = []
             for s in range(HALF_TILES // SLICE_TILES):
                 hnew_grouped = halves.tile(
                     [P, SLICE, LANES], BF16, name="hnew_grouped%d_%d" % (half, s), align_bytes=64
                 )
-                nc.scalar.copy(
-                    out=hnew_grouped[:],
-                    in_=hnew[:, :, s * SLICE : (s + 1) * SLICE].rearrange("q t n -> q n t"),
-                )
+                by_node = hnew[:, :, s * SLICE : (s + 1) * SLICE].rearrange("q t n -> q n t")
+                if s == 0:
+                    nc.scalar.copy(out=hnew_grouped[:], in_=by_node)
+                else:
+                    nc.gpsimd.tensor_scalar(
+                        out=hnew_grouped[:],
+                        in0=by_node,
+                        scalar1=1.0,
+                        scalar2=0.0,
+                        op0=ALU.mult,
+                        op1=ALU.add,
+                    )
                 grouped.append(hnew_grouped)
             return grouped
 
-        def readout(half, grouped):
-            out_banks = []
-            for s in range(HALF_TILES // SLICE_TILES):
-                hnew_codes = work.tile([P, SLICE], U32, align_bytes=64)
-                hnew_scales = work.tile([P, SLICE], U8, align_bytes=64)
-                nc.vector.quantize_mx(
-                    out=hnew_codes[:].bitcast(FP8X4),
-                    scales=hnew_scales[:],
-                    in_=grouped[s][:].rearrange("q n t -> q (n t)"),
+        def readout_matmuls(hnew_grouped):
+            hnew_codes = work.tile([P, SLICE], U32, align_bytes=64)
+            hnew_scales = work.tile([P, SLICE], U8, align_bytes=64)
+            nc.vector.quantize_mx(
+                out=hnew_codes[:].bitcast(FP8X4),
+                scales=hnew_scales[:],
+                in_=hnew_grouped[:].rearrange("q n t -> q (n t)"),
+            )
+            out_bank = psum_pairs.tile([P, SLICE_TILES, OUTPUTS], F32, tag="pair")
+            for j in range(SLICE_TILES):
+                tile_nodes = slice(j * P, (j + 1) * P)
+                nc.tensor.matmul_mx(
+                    out=out_bank[:, j, :],
+                    lhsT=hnew_codes[:, tile_nodes].bitcast(FP8X4),
+                    lhsT_scale=hnew_scales[:, tile_nodes],
+                    rhs=w_codes[:].bitcast(FP8X4),
+                    rhs_scale=w_scales[:],
+                    start=True,
+                    stop=True,
                 )
-                out_bank = psum_out.tile([P, SLICE_TILES, OUTPUTS], F32)
-                for j in range(SLICE_TILES):
-                    tile_nodes = slice(j * P, (j + 1) * P)
-                    nc.tensor.matmul_mx(
-                        out=out_bank[:, j, :],
-                        lhsT=hnew_codes[:, tile_nodes].bitcast(FP8X4),
-                        lhsT_scale=hnew_scales[:, tile_nodes],
-                        rhs=w_codes[:].bitcast(FP8X4),
-                        rhs_scale=w_scales[:],
-                        start=True,
-                        stop=True,
-                    )
-                out_banks.append(out_bank)
-            for s in range(HALF_TILES // SLICE_TILES):
-                out_sb = work.tile([P, SLICE_TILES, OUTPUTS], F32)
-                nc.vector.tensor_tensor(
-                    out=out_sb[:],
-                    in0=out_banks[s][:],
-                    in1=dense_bias[:].unsqueeze(1).to_broadcast([P, SLICE_TILES, OUTPUTS]),
-                    op=ALU.add,
-                )
-                first_tile = half * HALF_TILES + s * SLICE_TILES
-                nc.sync.dma_start(
-                    out=out_rows[:, first_tile : first_tile + SLICE_TILES, :], in_=out_sb[:]
-                )
+            return out_bank
 
-        quantise_u(Z)
+        def store_result(half, s, out_bank):
+            out_sb = results.tile([P, SLICE_TILES, OUTPUTS], F32)
+            nc.vector.tensor_tensor(
+                out=out_sb[:],
+                in0=out_bank[:],
+                in1=dense_bias[:].unsqueeze(1).to_broadcast([P, SLICE_TILES, OUTPUTS]),
+                op=ALU.add,
+            )
+            first_tile = half * HALF_TILES + s * SLICE_TILES
+            nc.sync.dma_start(out=out_rows[:, first_tile : first_tile + SLICE_TILES, :], in_=out_sb[:])
+
+
+        def transposed_candidate_gx(half):
+            x_banks = []
+            for u in range(BLOCKS):
+                x_banks.append(transposed_gx(half, CAND, u))
+            return x_banks
+
         h_lanes = transposed_h(0)
-        x_words_z = gx_words_in_sbuf(0, Z)
+        u_grouped = [group_u(Z, on_gpsimd=False), group_u(R, on_gpsimd=True), group_u(CAND, on_gpsimd=True)]
         h_mx = quantise_h(0, h_lanes)
+        quantise_u(Z, u_grouped[Z])
+        x_words_z = gx_words_in_sbuf(0, Z)
 
         bias_bank = psum_words.tile([P, HALF], F32, tag="words")
         nc.tensor.transpose(bias_bank[:, 0:P], bias_rows[:].bitcast(F32), ident[:])
         gate_bias = const.tile([P, GATES * LANES], F32)
         nc.vector.tensor_copy(out=gate_bias[:], in_=bias_bank[:, 0 : GATES * BLOCKS].bitcast(BF16))
 
-        quantise_u(R)
-
         w_grouped = weights.tile([P, OUTPUTS, LANES], BF16, align_bytes=64)
         nc.scalar.copy(out=w_grouped[:], in_=w_raw[:].rearrange("k t w -> k w t"))
         w_codes = weights.tile([P, OUTPUTS], U32, align_bytes=64)
         w_scales = weights.tile([P, OUTPUTS], U8, align_bytes=64)
-        nc.vector.quantize_mx(
-            out=w_codes[:].bitcast(FP8X4),
-            scales=w_scales[:],
-            in_=w_grouped[:].rearrange("k w t -> k (w t)"),
-        )
 
         for half in range(HALVES):
-            z = sigmoid_gate(half, Z, h_mx, x_words_z)
-            kept = kept_state(half, z, h_lanes)
-            x_words_r = gx_words_in_sbuf(half, R)
-            x_banks = []
-            for u in range(BLOCKS):
-                x_banks.append(transposed_gx(half, CAND, u))
-            if half == 0:
-                quantise_u(CAND)
-            else:
-                readout(half - 1, grouped)
-            r = sigmoid_gate(half, R, h_mx, x_words_r)
-            cand = candidate(half, h_mx, x_banks, r)
-            if half + 1 < HALVES:
+            is_first = half == 0
+            is_last = half == HALVES - 1
+            z = gate_sums(half, Z, h_mx, x_words_z)
+            if is_first:
+                x_words_r = gx_words_in_sbuf(half, R)
+                x_banks = transposed_candidate_gx(half)
+            sigmoid_in_place(z)
+            z_minus_1, kept = kept_state(half, z, h_lanes)
+            if is_first:
+                quantise_u(R, u_grouped[R])
+                quantise_u(CAND, u_grouped[CAND])
+            r = gate_sums(half, R, h_mx, x_words_r)
+            sigmoid_in_place(r)
+
+            cand = halves.tile([P, LANES, HALF], F32, name="cand%d" % half)
+            candidate_block(cand, 0, h_mx, x_banks[0], r)
+            minus_new_01 = work.tile([P, PAIR, HALF], F32, tag="minus_new")
+            nc.gpsimd.tensor_tensor(
+                out=minus_new_01[:], in0=z_minus_1[:], in1=cand[:, 0:PAIR, :], op=ALU.mult
+            )
+            if not is_last:
                 h_lanes = transposed_h(half + 1)
-                x_words_z = gx_words_in_sbuf(half + 1, Z)
-            grouped = new_state(half, z, kept, cand)
-            if half + 1 < HALVES:
+            candidate_block(cand, 1, h_mx, x_banks[1], r)
+
+            if is_last:
+                out_banks = []
+                for s in range(HALF_TILES // SLICE_TILES):
+                    out_banks.append(readout_matmuls(grouped[s]))
+            else:
                 h_mx = quantise_h(half + 1, h_lanes)
-        readout(HALVES - 1, grouped)
+                nc.vector.quantize_mx(
+                    out=w_codes[:].bitcast(FP8X4),
+                    scales=w_scales[:],
+                    in_=w_grouped[:].rearrange("k w t -> k (w t)"),
+                )
+                x_words_z = gx_words_in_sbuf(half + 1, Z)
+                x_words_r = gx_words_in_sbuf(half + 1, R)
+                x_banks = transposed_candidate_gx(half + 1)
+
+            minus_new_23 = work.tile([P, PAIR, HALF], F32, tag="minus_new")
+            nc.vector.scalar_tensor_tensor(
+                out=minus_new_23[:],
+                in0=z[:, PAIR:LANES, :],
+                scalar=1.0,
+                in1=cand[:, PAIR:LANES, :],
+                op0=ALU.subtract,
+                op1=ALU.mult,
+            )
+            hnew = halves.tile([P, LANES, HALF], BF16, name="hnew%d" % half)
+            nc.vector.tensor_tensor(
+                out=hnew[:, 0:PAIR, :], in0=kept[:, 0:PAIR, :], in1=minus_new_01[:], op=ALU.subtract
+            )
+            nc.vector.tensor_tensor(
+                out=hnew[:, PAIR:LANES, :], in0=kept[:, PAIR:LANES, :], in1=minus_new_23[:], op=ALU.subtract
+            )
+            grouped = group_new_state(half, hnew)
+
+        for s in range(HALF_TILES // SLICE_TILES):
+            store_result(HALVES - 2, s, out_banks[s])
+        out_banks = []
+        for s in range(HALF_TILES // SLICE_TILES):
+            out_banks.append(readout_matmuls(grouped[s]))
+        for s in range(HALF_TILES // SLICE_TILES):
+            store_result(HALVES - 1, s, out_banks[s])

@@ -124,25 +124,21 @@ def tile_gatedgraphconvolution_pb_kernel(
             u_codes.append(weights.tile([P, CHANNELS], U32, name="u_codes%d" % gate, align_bytes=64))
             u_scales.append(weights.tile([P, CHANNELS], U8, name="u_scales%d" % gate, align_bytes=64))
 
-        def group_u(gate, on_gpsimd):
+        def gpsimd_copy(out, in_):
+            nc.gpsimd.tensor_scalar(
+                out=out, in0=in_, scalar1=1.0, scalar2=0.0, op0=ALU.mult, op1=ALU.add
+            )
+
+        def group_u(gate, copy):
             u_grouped = weights.tile(
                 [P, CHANNELS, LANES], BF16, name="u_grouped%d" % gate, align_bytes=64
             )
             for u in range(BLOCKS):
                 block = slice(PAIR * P * u, PAIR * P * (u + 1))
-                sorted_columns = u_grouped[:, block, :].rearrange("k (e q) t -> k e q t", e=PAIR)
-                columns = u_raw[gate][:, :, block].rearrange("k t (q e) -> k e q t", e=PAIR)
-                if on_gpsimd:
-                    nc.gpsimd.tensor_scalar(
-                        out=sorted_columns,
-                        in0=columns,
-                        scalar1=1.0,
-                        scalar2=0.0,
-                        op0=ALU.mult,
-                        op1=ALU.add,
-                    )
-                else:
-                    nc.vector.tensor_copy(out=sorted_columns, in_=columns)
+                copy(
+                    out=u_grouped[:, block, :].rearrange("k (e q) t -> k e q t", e=PAIR),
+                    in_=u_raw[gate][:, :, block].rearrange("k t (q e) -> k e q t", e=PAIR),
+                )
             return u_grouped
 
         def quantise_u(gate, u_grouped):
@@ -244,14 +240,7 @@ def tile_gatedgraphconvolution_pb_kernel(
 
         def kept_state(half, z, h_lanes):
             z_minus_1 = halves.tile([P, PAIR, HALF], F32, name="z_minus_1_%d" % half)
-            nc.gpsimd.tensor_scalar(
-                out=z_minus_1[:],
-                in0=z[:, 0:PAIR, :],
-                scalar1=1.0,
-                scalar2=-1.0,
-                op0=ALU.mult,
-                op1=ALU.add,
-            )
+            nc.scalar.add(out=z_minus_1[:], in_=z[:, 0:PAIR, :], add=-1.0)
             kept = halves.tile([P, LANES, HALF], F32, name="kept%d" % half)
             h_by_lane = h_lanes.rearrange("q (n t) -> q t n", t=LANES)
             for u in range(BLOCKS):
@@ -271,25 +260,24 @@ def tile_gatedgraphconvolution_pb_kernel(
                 if s == 0:
                     nc.scalar.copy(out=hnew_grouped[:], in_=by_node)
                 else:
-                    nc.gpsimd.tensor_scalar(
-                        out=hnew_grouped[:],
-                        in0=by_node,
-                        scalar1=1.0,
-                        scalar2=0.0,
-                        op0=ALU.mult,
-                        op1=ALU.add,
-                    )
+                    gpsimd_copy(out=hnew_grouped[:], in_=by_node)
                 grouped.append(hnew_grouped)
             return grouped
 
-        def readout_matmuls(hnew_grouped):
-            hnew_codes = work.tile([P, SLICE], U32, align_bytes=64)
-            hnew_scales = work.tile([P, SLICE], U8, align_bytes=64)
-            nc.vector.quantize_mx(
-                out=hnew_codes[:].bitcast(FP8X4),
-                scales=hnew_scales[:],
-                in_=hnew_grouped[:].rearrange("q n t -> q (n t)"),
-            )
+        def quantise_new_state(grouped):
+            hnew_mx = []
+            for s in range(HALF_TILES // SLICE_TILES):
+                hnew_codes = work.tile([P, SLICE], U32, align_bytes=64)
+                hnew_scales = work.tile([P, SLICE], U8, align_bytes=64)
+                nc.vector.quantize_mx(
+                    out=hnew_codes[:].bitcast(FP8X4),
+                    scales=hnew_scales[:],
+                    in_=grouped[s][:].rearrange("q n t -> q (n t)"),
+                )
+                hnew_mx.append((hnew_codes, hnew_scales))
+            return hnew_mx
+
+        def readout_matmuls(hnew_codes, hnew_scales):
             out_bank = psum_pairs.tile([P, SLICE_TILES, OUTPUTS], F32, tag="pair")
             for j in range(SLICE_TILES):
                 tile_nodes = slice(j * P, (j + 1) * P)
@@ -323,7 +311,11 @@ def tile_gatedgraphconvolution_pb_kernel(
             return x_banks
 
         h_lanes = transposed_h(0)
-        u_grouped = [group_u(Z, on_gpsimd=False), group_u(R, on_gpsimd=True), group_u(CAND, on_gpsimd=True)]
+        u_grouped = [
+            group_u(Z, nc.vector.tensor_copy),
+            group_u(R, nc.scalar.copy),
+            group_u(CAND, gpsimd_copy),
+        ]
         h_mx = quantise_h(0, h_lanes)
         quantise_u(Z, u_grouped[Z])
         x_words_z = gx_words_in_sbuf(0, Z)
@@ -350,8 +342,14 @@ def tile_gatedgraphconvolution_pb_kernel(
             if is_first:
                 quantise_u(R, u_grouped[R])
                 quantise_u(CAND, u_grouped[CAND])
+            else:
+                hnew_mx = quantise_new_state(grouped)
             r = gate_sums(half, R, h_mx, x_words_r)
             sigmoid_in_place(r)
+            if not is_first:
+                out_banks = []
+                for s in range(HALF_TILES // SLICE_TILES):
+                    out_banks.append(readout_matmuls(*hnew_mx[s]))
 
             cand = halves.tile([P, LANES, HALF], F32, name="cand%d" % half)
             candidate_block(cand, 0, h_mx, x_banks[0], r)
@@ -364,9 +362,7 @@ def tile_gatedgraphconvolution_pb_kernel(
             candidate_block(cand, 1, h_mx, x_banks[1], r)
 
             if is_last:
-                out_banks = []
-                for s in range(HALF_TILES // SLICE_TILES):
-                    out_banks.append(readout_matmuls(grouped[s]))
+                store_result(half - 1, 0, out_banks[0])
             else:
                 h_mx = quantise_h(half + 1, h_lanes)
                 nc.vector.quantize_mx(
@@ -396,10 +392,7 @@ def tile_gatedgraphconvolution_pb_kernel(
             )
             grouped = group_new_state(half, hnew)
 
+        store_result(HALVES - 2, 1, out_banks[1])
+        hnew_mx = quantise_new_state(grouped)
         for s in range(HALF_TILES // SLICE_TILES):
-            store_result(HALVES - 2, s, out_banks[s])
-        out_banks = []
-        for s in range(HALF_TILES // SLICE_TILES):
-            out_banks.append(readout_matmuls(grouped[s]))
-        for s in range(HALF_TILES // SLICE_TILES):
-            store_result(HALVES - 1, s, out_banks[s])
+            store_result(HALVES - 1, s, readout_matmuls(*hnew_mx[s]))

@@ -26,14 +26,26 @@ NODE_TILES = NODES // P
 HALVES = 2
 HALF_TILES = NODE_TILES // HALVES
 HALF = HALF_TILES * P
-SLICE_TILES = 2
-SLICE = SLICE_TILES * P
+READ_TILES = 2
+LAST_SLICES = (256, 256)
 
 FLOPS = 2 * NODES * CHANNELS * (GATES * CHANNELS + OUTPUTS)
 
 
 def lane_of_words(words, e):
     return words.bitcast(BF16).rearrange("p (n e) -> p n e", e=PAIR)[:, :, e]
+
+
+def pairs_of_words(words):
+    return words.bitcast(BF16).rearrange("p (n e) -> p n e", e=PAIR)
+
+
+def lanes_of_block(u):
+    return slice(PAIR * u, PAIR * (u + 1))
+
+
+def lanes_range(u):
+    return range(PAIR * u, PAIR * (u + 1))
 
 
 def tile_gatedgraphconvolution_pb_kernel(
@@ -49,8 +61,6 @@ def tile_gatedgraphconvolution_pb_kernel(
         inputs = ctx.enter_context(tc.tile_pool(name="inputs", bufs=1))
         weights = ctx.enter_context(tc.tile_pool(name="weights", bufs=1))
         halves = ctx.enter_context(tc.tile_pool(name="halves", bufs=1))
-        work = ctx.enter_context(tc.tile_pool(name="work", bufs=2))
-        results = ctx.enter_context(tc.tile_pool(name="results", bufs=4))
         psum_gh = ctx.enter_context(tc.psum_pool(name="psum_gh", bufs=3))
         psum_words = ctx.enter_context(tc.psum_pool(name="psum_words", bufs=3))
         psum_pairs = ctx.enter_context(tc.psum_pool(name="psum_pairs", bufs=2))
@@ -72,17 +82,17 @@ def tile_gatedgraphconvolution_pb_kernel(
         bias_rows = const.tile([P, PAIR * P], BF16)
         dense_bias = const.tile([P, OUTPUTS], BF16)
 
-        def load_lanes(queue, raw, rows):
+        def load_lanes(raw, rows):
             for u in range(BLOCKS):
-                queue.dma_start(
-                    out=raw[:, PAIR * u : PAIR * (u + 1), :],
+                nc.sync.dma_start(
+                    out=raw[:, lanes_of_block(u), :],
                     in_=rows[PAIR * P * u : PAIR * P * (u + 1), :].rearrange(
                         "(q e) w -> q e w", e=PAIR
                     ),
                 )
 
         def load_u(gate):
-            load_lanes(nc.sync, u_raw[gate], gru_U[:, gate * CHANNELS : (gate + 1) * CHANNELS])
+            load_lanes(u_raw[gate], gru_U[:, gate * CHANNELS : (gate + 1) * CHANNELS])
 
         def load_h(half):
             tiles = slice(half * HALF_TILES, (half + 1) * HALF_TILES)
@@ -93,22 +103,19 @@ def tile_gatedgraphconvolution_pb_kernel(
             cols = slice(gate * CHANNELS, (gate + 1) * CHANNELS)
             nc.sync.dma_start(out=gx_sb[half][gate][:], in_=gx_rows[:, tiles, cols])
 
+        load_h(0)
         nc.vector.memset(bias_rows[:], 0.0)
-        nc.scalar.dma_start(
+        nc.sync.dma_start(
             out=bias_rows[0 : GATES * BLOCKS, :],
             in_=gru_b_h.rearrange("(r c) -> r c", c=PAIR * P),
         )
-        load_lanes(nc.scalar, w_raw, dense_W)
-        load_h(0)
-        load_u(Z)
-        load_u(R)
-        load_gx(0, Z)
-        load_u(CAND)
-        load_gx(0, R)
-        load_gx(0, CAND)
+        for gate in range(GATES):
+            load_u(gate)
+            load_gx(0, gate)
         load_h(1)
         for gate in range(GATES):
             load_gx(1, gate)
+        load_lanes(w_raw, dense_W)
         nc.sync.dma_start(out=dense_bias[:], in_=dense_b.partition_broadcast(P))
 
         ident = const.tile([P, P], F32)
@@ -118,34 +125,47 @@ def tile_gatedgraphconvolution_pb_kernel(
         nc.vector.memset(warm[:], 0.0)
         nc.scalar.activation(out=warm[:], in_=warm[:], func=ACT.Sigmoid)
 
+        u_grouped = []
         u_codes = []
         u_scales = []
         for gate in range(GATES):
+            u_grouped.append(
+                weights.tile([P, CHANNELS, LANES], BF16, name="u_grouped%d" % gate, align_bytes=64)
+            )
             u_codes.append(weights.tile([P, CHANNELS], U32, name="u_codes%d" % gate, align_bytes=64))
             u_scales.append(weights.tile([P, CHANNELS], U8, name="u_scales%d" % gate, align_bytes=64))
+        w_grouped = weights.tile([P, OUTPUTS, LANES], BF16, align_bytes=64)
+        w_codes = weights.tile([P, OUTPUTS], U32, align_bytes=64)
+        w_scales = weights.tile([P, OUTPUTS], U8, align_bytes=64)
 
         def gpsimd_copy(out, in_):
             nc.gpsimd.tensor_scalar(
                 out=out, in0=in_, scalar1=1.0, scalar2=0.0, op0=ALU.mult, op1=ALU.add
             )
 
-        def group_u(gate, copy):
-            u_grouped = weights.tile(
-                [P, CHANNELS, LANES], BF16, name="u_grouped%d" % gate, align_bytes=64
+        def group_u(gate, u, copy):
+            block = slice(PAIR * P * u, PAIR * P * (u + 1))
+            copy(
+                out=u_grouped[gate][:, block, :].rearrange("k (e q) t -> k e q t", e=PAIR),
+                in_=u_raw[gate][:, :, block].rearrange("k t (q e) -> k e q t", e=PAIR),
             )
-            for u in range(BLOCKS):
-                block = slice(PAIR * P * u, PAIR * P * (u + 1))
-                copy(
-                    out=u_grouped[:, block, :].rearrange("k (e q) t -> k e q t", e=PAIR),
-                    in_=u_raw[gate][:, :, block].rearrange("k t (q e) -> k e q t", e=PAIR),
-                )
-            return u_grouped
 
-        def quantise_u(gate, u_grouped):
+        def quantise_u(gate, first=0, count=CHANNELS):
+            positions = slice(first, first + count)
             nc.vector.quantize_mx(
-                out=u_codes[gate][:].bitcast(FP8X4),
-                scales=u_scales[gate][:],
-                in_=u_grouped[:].rearrange("k w t -> k (w t)"),
+                out=u_codes[gate][:, positions].bitcast(FP8X4),
+                scales=u_scales[gate][:, positions],
+                in_=u_grouped[gate][:, positions, :].rearrange("k w t -> k (w t)"),
+            )
+
+        def group_w():
+            nc.scalar.copy(out=w_grouped[:], in_=w_raw[:].rearrange("k t w -> k w t"))
+
+        def quantise_w():
+            nc.vector.quantize_mx(
+                out=w_codes[:].bitcast(FP8X4),
+                scales=w_scales[:],
+                in_=w_grouped[:].rearrange("k w t -> k (w t)"),
             )
 
         def transposed_gx(half, gate, u):
@@ -158,26 +178,38 @@ def tile_gatedgraphconvolution_pb_kernel(
                 )
             return bank
 
-        def gx_words_in_sbuf(half, gate):
+        def transposed_gx_blocks(half, gate):
+            banks = []
+            for u in range(BLOCKS):
+                banks.append(transposed_gx(half, gate, u))
+            return banks
+
+        def words_in_sbuf(half, gate, banks):
             x_words = halves.tile([P, BLOCKS, HALF], F32, name="x_words%d_%d" % (half, gate))
             for u in range(BLOCKS):
-                nc.scalar.copy(out=x_words[:, u, :], in_=transposed_gx(half, gate, u)[:])
+                nc.scalar.copy(out=x_words[:, u, :], in_=banks[u][:])
             return x_words
 
         def transposed_h(half):
-            h_words = halves.tile([P, HALF, BLOCKS], F32, name="h_words%d" % half, align_bytes=64)
-            for s in range(HALF_TILES // SLICE_TILES):
-                bank = psum_pairs.tile([P, BLOCKS, SLICE], F32, tag="pair")
+            banks = []
+            for s in range(HALF_TILES // PAIR):
+                bank = psum_pairs.tile([P, BLOCKS, PAIR * P], F32, tag="pair")
                 for u in range(BLOCKS):
-                    for j in range(SLICE_TILES):
+                    for j in range(PAIR):
                         nc.tensor.transpose(
                             bank[:, u, j * P : (j + 1) * P],
-                            h_sb[half][:, s * SLICE_TILES + j, :].bitcast(F32)[:, u * P : (u + 1) * P],
+                            h_sb[half][:, PAIR * s + j, :].bitcast(F32)[:, u * P : (u + 1) * P],
                             ident[:],
                         )
+                banks.append(bank)
+            return banks
+
+        def h_in_sbuf(half, banks):
+            h_words = halves.tile([P, HALF, BLOCKS], F32, name="h_words%d" % half, align_bytes=64)
+            for s in range(HALF_TILES // PAIR):
                 nc.scalar.copy(
-                    out=h_words[:, s * SLICE : (s + 1) * SLICE, :],
-                    in_=bank[:].rearrange("q u n -> q n u"),
+                    out=h_words[:, s * PAIR * P : (s + 1) * PAIR * P, :],
+                    in_=banks[s][:].rearrange("q u n -> q n u"),
                 )
             return h_words[:].rearrange("q n u -> q (n u)").bitcast(BF16)
 
@@ -187,212 +219,259 @@ def tile_gatedgraphconvolution_pb_kernel(
             nc.vector.quantize_mx(out=h_codes[:].bitcast(FP8X4), scales=h_scales[:], in_=h_lanes)
             return h_codes, h_scales
 
-        def gh_bank(h_mx, gate, t):
+        def gh_banks(h_mx, gate, first=0, count=HALF):
             h_codes, h_scales = h_mx
-            bank = psum_gh.tile([P, HALF], F32, tag="gh")
-            positions = slice(t * P, (t + 1) * P)
-            nc.tensor.matmul_mx(
-                out=bank[:],
-                lhsT=u_codes[gate][:, positions].bitcast(FP8X4),
-                lhsT_scale=u_scales[gate][:, positions],
-                rhs=h_codes[:].bitcast(FP8X4),
-                rhs_scale=h_scales[:],
-                start=True,
-                stop=True,
-            )
-            return bank
-
-        def gate_sums(half, gate, h_mx, x_words):
-            sums = halves.tile([P, LANES, HALF], F32, name="gate%d_%d" % (half, gate))
+            nodes = slice(first, first + count)
+            in_bank = HALF // count
+            lanes = []
             for t in range(LANES):
-                nc.vector.scalar_tensor_tensor(
-                    out=sums[:, t, :],
-                    in0=gh_bank(h_mx, gate, t)[:],
-                    scalar=gate_bias[:, gate * LANES + t : gate * LANES + t + 1],
-                    in1=lane_of_words(x_words[:, t // PAIR, :], t % PAIR),
-                    op0=ALU.add,
-                    op1=ALU.add,
-                )
-            return sums
-
-        def sigmoid_in_place(sums):
-            for t in range(LANES):
-                nc.scalar.activation(out=sums[:, t, :], in_=sums[:, t, :], func=ACT.Sigmoid)
-
-        def candidate_block(cand, u, h_mx, x_bank, r):
-            for t in range(PAIR * u, PAIR * (u + 1)):
-                nc.vector.scalar_tensor_tensor(
-                    out=cand[:, t, :],
-                    in0=gh_bank(h_mx, CAND, t)[:],
-                    scalar=gate_bias[:, CAND * LANES + t : CAND * LANES + t + 1],
-                    in1=r[:, t, :],
-                    op0=ALU.add,
-                    op1=ALU.mult,
-                )
-            for t in range(PAIR * u, PAIR * (u + 1)):
-                nc.vector.tensor_tensor(
-                    out=cand[:, t, :],
-                    in0=cand[:, t, :],
-                    in1=lane_of_words(x_bank[:], t % PAIR),
-                    op=ALU.add,
-                )
-                nc.scalar.activation(out=cand[:, t, :], in_=cand[:, t, :], func=ACT.Tanh)
-
-        def kept_state(half, z, h_lanes):
-            z_minus_1 = halves.tile([P, PAIR, HALF], F32, name="z_minus_1_%d" % half)
-            nc.scalar.add(out=z_minus_1[:], in_=z[:, 0:PAIR, :], add=-1.0)
-            kept = halves.tile([P, LANES, HALF], F32, name="kept%d" % half)
-            h_by_lane = h_lanes.rearrange("q (n t) -> q t n", t=LANES)
-            for u in range(BLOCKS):
-                lanes = slice(PAIR * u, PAIR * (u + 1))
-                nc.gpsimd.tensor_tensor(
-                    out=kept[:, lanes, :], in0=z[:, lanes, :], in1=h_by_lane[:, lanes, :], op=ALU.mult
-                )
-            return z_minus_1, kept
-
-        def group_new_state(half, hnew):
-            grouped = []
-            for s in range(HALF_TILES // SLICE_TILES):
-                hnew_grouped = halves.tile(
-                    [P, SLICE, LANES], BF16, name="hnew_grouped%d_%d" % (half, s), align_bytes=64
-                )
-                by_node = hnew[:, :, s * SLICE : (s + 1) * SLICE].rearrange("q t n -> q n t")
-                if s == 0:
-                    nc.scalar.copy(out=hnew_grouped[:], in_=by_node)
-                else:
-                    gpsimd_copy(out=hnew_grouped[:], in_=by_node)
-                grouped.append(hnew_grouped)
-            return grouped
-
-        def quantise_new_state(grouped):
-            hnew_mx = []
-            for s in range(HALF_TILES // SLICE_TILES):
-                hnew_codes = work.tile([P, SLICE], U32, align_bytes=64)
-                hnew_scales = work.tile([P, SLICE], U8, align_bytes=64)
-                nc.vector.quantize_mx(
-                    out=hnew_codes[:].bitcast(FP8X4),
-                    scales=hnew_scales[:],
-                    in_=grouped[s][:].rearrange("q n t -> q (n t)"),
-                )
-                hnew_mx.append((hnew_codes, hnew_scales))
-            return hnew_mx
-
-        def readout_matmuls(hnew_codes, hnew_scales):
-            out_bank = psum_pairs.tile([P, SLICE_TILES, OUTPUTS], F32, tag="pair")
-            for j in range(SLICE_TILES):
-                tile_nodes = slice(j * P, (j + 1) * P)
+                if t % in_bank == 0:
+                    bank = psum_gh.tile([P, HALF], F32, tag="gh")
+                place = t % in_bank * count
+                positions = slice(t * P, (t + 1) * P)
                 nc.tensor.matmul_mx(
-                    out=out_bank[:, j, :],
-                    lhsT=hnew_codes[:, tile_nodes].bitcast(FP8X4),
-                    lhsT_scale=hnew_scales[:, tile_nodes],
+                    out=bank[:, place : place + count],
+                    lhsT=u_codes[gate][:, positions].bitcast(FP8X4),
+                    lhsT_scale=u_scales[gate][:, positions],
+                    rhs=h_codes[:, nodes].bitcast(FP8X4),
+                    rhs_scale=h_scales[:, nodes],
+                    start=True,
+                    stop=True,
+                )
+                lanes.append(bank[:, place : place + count])
+            return lanes
+
+        def bias_of(gate, t):
+            return gate_bias[:, gate * LANES + t : gate * LANES + t + 1]
+
+        def add_gate_sum(sums, gate, t, gh_lanes, x_words):
+            nc.vector.scalar_tensor_tensor(
+                out=sums[:, t, :],
+                in0=gh_lanes[t],
+                scalar=bias_of(gate, t),
+                in1=lane_of_words(x_words[:, t // PAIR, :], t % PAIR),
+                op0=ALU.add,
+                op1=ALU.add,
+            )
+
+        def sigmoid_z(z, sums, u):
+            nc.scalar.activation(
+                out=z[:, u, :, :],
+                in_=sums[:, lanes_of_block(u), :].rearrange("q e n -> q n e"),
+                func=ACT.Sigmoid,
+            )
+
+        def sigmoid_r(sums, t):
+            nc.scalar.activation(out=sums[:, t, :], in_=sums[:, t, :], func=ACT.Sigmoid)
+
+        def keep_state(kept, z, h_lanes, u):
+            h_pairs = h_lanes.rearrange("q (n u e) -> q u n e", u=BLOCKS, e=PAIR)
+            for part in range(PAIR):
+                nodes = slice(part * HALF // PAIR, (part + 1) * HALF // PAIR)
+                nc.gpsimd.tensor_tensor(
+                    out=kept[:, u, nodes, :],
+                    in0=z[:, u, nodes, :],
+                    in1=h_pairs[:, u, nodes, :],
+                    op=ALU.mult,
+                )
+
+        def reset_product(products, t, gh_lanes, r, first, count):
+            nc.vector.scalar_tensor_tensor(
+                out=products[:, t, :],
+                in0=gh_lanes[t],
+                scalar=bias_of(CAND, t),
+                in1=r[:, t, first : first + count],
+                op0=ALU.add,
+                op1=ALU.mult,
+            )
+
+        def candidate_sum(cand, products, u, x_bank, first, count):
+            nc.vector.tensor_tensor(
+                out=cand[:, u, :, :],
+                in0=products[:, lanes_of_block(u), :].rearrange("q e n -> q n e"),
+                in1=pairs_of_words(x_bank[:, first : first + count]),
+                op=ALU.add,
+            )
+
+        def tanh_in_place(cand, u):
+            nc.scalar.activation(out=cand[:, u, :, :], in_=cand[:, u, :, :], func=ACT.Tanh)
+
+        def minus_new(product, z, cand, u, first, count):
+            nc.vector.scalar_tensor_tensor(
+                out=product[:, u, :, :],
+                in0=z[:, u, first : first + count, :],
+                scalar=1.0,
+                in1=cand[:, u, :, :],
+                op0=ALU.subtract,
+                op1=ALU.mult,
+            )
+
+        def by_node(paired):
+            return paired.rearrange("q u n e -> q n u e")
+
+        def new_state(engine, hnew, kept, product):
+            engine.tensor_tensor(
+                out=hnew.rearrange("q n (u e) -> q n u e", u=BLOCKS),
+                in0=by_node(kept),
+                in1=by_node(product),
+                op=ALU.subtract,
+            )
+
+        def quantise_new_state(name, hnew, count):
+            codes = halves.tile([P, count], U32, name="hnew_codes" + name, align_bytes=64)
+            scales = halves.tile([P, count], U8, name="hnew_scales" + name, align_bytes=64)
+            nc.vector.quantize_mx(
+                out=codes[:].bitcast(FP8X4),
+                scales=scales[:],
+                in_=hnew.rearrange("q n t -> q (n t)"),
+            )
+            return codes, scales
+
+        def readout(hnew_mx, tiles):
+            codes, scales = hnew_mx
+            bank = psum_pairs.tile([P, READ_TILES, OUTPUTS], F32, tag="pair")
+            for j in range(tiles):
+                nodes = slice(j * P, (j + 1) * P)
+                nc.tensor.matmul_mx(
+                    out=bank[:, j, :],
+                    lhsT=codes[:, nodes].bitcast(FP8X4),
+                    lhsT_scale=scales[:, nodes],
                     rhs=w_codes[:].bitcast(FP8X4),
                     rhs_scale=w_scales[:],
                     start=True,
                     stop=True,
                 )
-            return out_bank
+            return bank
 
-        def store_result(half, s, out_bank):
-            out_sb = results.tile([P, SLICE_TILES, OUTPUTS], F32)
+        def store_result(name, first_tile, tiles, bank):
+            result = halves.tile([P, tiles, OUTPUTS], F32, name="result" + name)
             nc.vector.tensor_tensor(
-                out=out_sb[:],
-                in0=out_bank[:],
-                in1=dense_bias[:].unsqueeze(1).to_broadcast([P, SLICE_TILES, OUTPUTS]),
+                out=result[:],
+                in0=bank[:, 0:tiles, :],
+                in1=dense_bias[:].unsqueeze(1).to_broadcast([P, tiles, OUTPUTS]),
                 op=ALU.add,
             )
-            first_tile = half * HALF_TILES + s * SLICE_TILES
-            nc.sync.dma_start(out=out_rows[:, first_tile : first_tile + SLICE_TILES, :], in_=out_sb[:])
+            nc.sync.dma_start(out=out_rows[:, first_tile : first_tile + tiles, :], in_=result[:])
 
+        z = []
+        z_sums = []
+        r_sums = []
+        kept = []
+        for half in range(HALVES):
+            z.append(halves.tile([P, BLOCKS, HALF, PAIR], F32, name="z%d" % half))
+            z_sums.append(halves.tile([P, LANES, HALF], F32, name="z_sums%d" % half))
+            r_sums.append(halves.tile([P, LANES, HALF], F32, name="r_sums%d" % half))
+            kept.append(halves.tile([P, BLOCKS, HALF, PAIR], F32, name="kept%d" % half))
 
-        def transposed_candidate_gx(half):
-            x_banks = []
-            for u in range(BLOCKS):
-                x_banks.append(transposed_gx(half, CAND, u))
-            return x_banks
-
-        h_lanes = transposed_h(0)
-        u_grouped = [
-            group_u(Z, nc.vector.tensor_copy),
-            group_u(R, nc.scalar.copy),
-            group_u(CAND, gpsimd_copy),
-        ]
-        h_mx = quantise_h(0, h_lanes)
-        quantise_u(Z, u_grouped[Z])
-        x_words_z = gx_words_in_sbuf(0, Z)
+        h_banks0 = transposed_h(0)
 
         bias_bank = psum_words.tile([P, HALF], F32, tag="words")
         nc.tensor.transpose(bias_bank[:, 0:P], bias_rows[:].bitcast(F32), ident[:])
         gate_bias = const.tile([P, GATES * LANES], F32)
+
+        h_lanes0 = h_in_sbuf(0, h_banks0)
+        for u in range(BLOCKS):
+            group_u(Z, u, nc.vector.tensor_copy)
         nc.vector.tensor_copy(out=gate_bias[:], in_=bias_bank[:, 0 : GATES * BLOCKS].bitcast(BF16))
+        h_mx0 = quantise_h(0, h_lanes0)
+        quantise_u(Z, 0, CHANNELS // 2)
+        quantise_u(Z, CHANNELS // 2, CHANNELS // 2)
+        x_words = words_in_sbuf(0, Z, transposed_gx_blocks(0, Z))
+        group_u(R, 0, nc.scalar.copy)
+        group_u(R, 1, gpsimd_copy)
+        for u in range(BLOCKS):
+            group_u(CAND, u, gpsimd_copy)
 
-        w_grouped = weights.tile([P, OUTPUTS, LANES], BF16, align_bytes=64)
-        nc.scalar.copy(out=w_grouped[:], in_=w_raw[:].rearrange("k t w -> k w t"))
-        w_codes = weights.tile([P, OUTPUTS], U32, align_bytes=64)
-        w_scales = weights.tile([P, OUTPUTS], U8, align_bytes=64)
+        gh = gh_banks(h_mx0, Z)
+        for t in range(LANES - 1):
+            add_gate_sum(z_sums[0], Z, t, gh, x_words)
+        quantise_u(R)
+        add_gate_sum(z_sums[0], Z, LANES - 1, gh, x_words)
+        x_words = words_in_sbuf(0, R, transposed_gx_blocks(0, R))
+        for u in range(BLOCKS):
+            sigmoid_z(z[0], z_sums[0], u)
+            keep_state(kept[0], z[0], h_lanes0, u)
 
-        for half in range(HALVES):
-            is_first = half == 0
-            is_last = half == HALVES - 1
-            z = gate_sums(half, Z, h_mx, x_words_z)
-            if is_first:
-                x_words_r = gx_words_in_sbuf(half, R)
-                x_banks = transposed_candidate_gx(half)
-            sigmoid_in_place(z)
-            z_minus_1, kept = kept_state(half, z, h_lanes)
-            if is_first:
-                quantise_u(R, u_grouped[R])
-                quantise_u(CAND, u_grouped[CAND])
-            else:
-                hnew_mx = quantise_new_state(grouped)
-            r = gate_sums(half, R, h_mx, x_words_r)
-            sigmoid_in_place(r)
-            if not is_first:
-                out_banks = []
-                for s in range(HALF_TILES // SLICE_TILES):
-                    out_banks.append(readout_matmuls(*hnew_mx[s]))
+        gh = gh_banks(h_mx0, R)
+        for t in range(LANES):
+            add_gate_sum(r_sums[0], R, t, gh, x_words)
+            sigmoid_r(r_sums[0], t)
+        quantise_u(CAND)
 
-            cand = halves.tile([P, LANES, HALF], F32, name="cand%d" % half)
-            candidate_block(cand, 0, h_mx, x_banks[0], r)
-            minus_new_01 = work.tile([P, PAIR, HALF], F32, tag="minus_new")
-            nc.gpsimd.tensor_tensor(
-                out=minus_new_01[:], in0=z_minus_1[:], in1=cand[:, 0:PAIR, :], op=ALU.mult
-            )
-            if not is_last:
-                h_lanes = transposed_h(half + 1)
-            candidate_block(cand, 1, h_mx, x_banks[1], r)
+        x_banks = transposed_gx_blocks(0, CAND)
+        gh = gh_banks(h_mx0, CAND)
+        h_lanes1 = h_in_sbuf(1, transposed_h(1))
+        products0 = halves.tile([P, LANES, HALF], F32)
+        cand0 = halves.tile([P, BLOCKS, HALF, PAIR], F32)
+        for t in lanes_range(0):
+            reset_product(products0, t, gh, r_sums[0], 0, HALF)
+        candidate_sum(cand0, products0, 0, x_banks[0], 0, HALF)
+        tanh_in_place(cand0, 0)
+        for t in lanes_range(1):
+            reset_product(products0, t, gh, r_sums[0], 0, HALF)
+        h_mx1 = quantise_h(1, h_lanes1)
+        candidate_sum(cand0, products0, 1, x_banks[1], 0, HALF)
+        x_words = words_in_sbuf(1, Z, transposed_gx_blocks(1, Z))
+        tanh_in_place(cand0, 1)
 
-            if is_last:
-                store_result(half - 1, 0, out_banks[0])
-            else:
-                h_mx = quantise_h(half + 1, h_lanes)
-                nc.vector.quantize_mx(
-                    out=w_codes[:].bitcast(FP8X4),
-                    scales=w_scales[:],
-                    in_=w_grouped[:].rearrange("k w t -> k (w t)"),
-                )
-                x_words_z = gx_words_in_sbuf(half + 1, Z)
-                x_words_r = gx_words_in_sbuf(half + 1, R)
-                x_banks = transposed_candidate_gx(half + 1)
+        gh = gh_banks(h_mx1, Z)
+        for t in lanes_range(0):
+            add_gate_sum(z_sums[1], Z, t, gh, x_words)
+        product0 = halves.tile([P, BLOCKS, HALF, PAIR], F32)
+        for u in range(BLOCKS):
+            minus_new(product0, z[0], cand0, u, 0, HALF)
+        for t in lanes_range(1):
+            add_gate_sum(z_sums[1], Z, t, gh, x_words)
+        x_words = words_in_sbuf(1, R, transposed_gx_blocks(1, R))
+        for u in range(BLOCKS):
+            sigmoid_z(z[1], z_sums[1], u)
 
-            minus_new_23 = work.tile([P, PAIR, HALF], F32, tag="minus_new")
-            nc.vector.scalar_tensor_tensor(
-                out=minus_new_23[:],
-                in0=z[:, PAIR:LANES, :],
-                scalar=1.0,
-                in1=cand[:, PAIR:LANES, :],
-                op0=ALU.subtract,
-                op1=ALU.mult,
-            )
-            hnew = halves.tile([P, LANES, HALF], BF16, name="hnew%d" % half)
-            nc.vector.tensor_tensor(
-                out=hnew[:, 0:PAIR, :], in0=kept[:, 0:PAIR, :], in1=minus_new_01[:], op=ALU.subtract
-            )
-            nc.vector.tensor_tensor(
-                out=hnew[:, PAIR:LANES, :], in0=kept[:, PAIR:LANES, :], in1=minus_new_23[:], op=ALU.subtract
-            )
-            grouped = group_new_state(half, hnew)
+        hnew0 = halves.tile([P, HALF, LANES], BF16, align_bytes=64)
+        for a in range(HALF_TILES):
+            nodes = slice(a * P, (a + 1) * P)
+            new_state(nc.gpsimd, hnew0[:, nodes, :], kept[0][:, :, nodes, :], product0[:, :, nodes, :])
+        for u in range(BLOCKS):
+            keep_state(kept[1], z[1], h_lanes1, u)
 
-        store_result(HALVES - 2, 1, out_banks[1])
-        hnew_mx = quantise_new_state(grouped)
-        for s in range(HALF_TILES // SLICE_TILES):
-            store_result(HALVES - 1, s, readout_matmuls(*hnew_mx[s]))
+        gh = gh_banks(h_mx1, R)
+        for t in range(LANES):
+            add_gate_sum(r_sums[1], R, t, gh, x_words)
+            sigmoid_r(r_sums[1], t)
+        group_w()
+
+        x_banks = transposed_gx_blocks(1, CAND)
+        slices = []
+        first = 0
+        for count in LAST_SLICES:
+            gh = gh_banks(h_mx1, CAND, first, count)
+            products = halves.tile([P, LANES, count], F32, name="products1_%d" % first)
+            cand = halves.tile([P, BLOCKS, count, PAIR], F32, name="cand1_%d" % first)
+            for u in range(BLOCKS):
+                for t in lanes_range(u):
+                    reset_product(products, t, gh, r_sums[1], first, count)
+                candidate_sum(cand, products, u, x_banks[u], first, count)
+                tanh_in_place(cand, u)
+            slices.append((first, count, cand))
+            first += count
+
+        quantise_w()
+        half0_banks = []
+        for s in range(HALF_TILES // READ_TILES):
+            nodes = slice(s * READ_TILES * P, (s + 1) * READ_TILES * P)
+            hnew_mx = quantise_new_state("0_%d" % s, hnew0[:, nodes, :], READ_TILES * P)
+            half0_banks.append(readout(hnew_mx, READ_TILES))
+        store_result("0_0", 0, READ_TILES, half0_banks[0])
+
+        hnew_mx1 = []
+        for first, count, cand in slices:
+            product = halves.tile([P, BLOCKS, count, PAIR], F32, name="product1_%d" % first)
+            hnew = halves.tile([P, count, LANES], BF16, name="hnew1_%d" % first, align_bytes=64)
+            for u in range(BLOCKS):
+                minus_new(product, z[1], cand, u, first, count)
+            new_state(nc.vector, hnew[:], kept[1][:, :, first : first + count, :], product[:])
+            hnew_mx1.append(quantise_new_state("1_%d" % first, hnew[:], count))
+            if first == 0:
+                store_result("0_1", READ_TILES, READ_TILES, half0_banks[1])
+        for (first, count, cand), hnew_mx in zip(slices, hnew_mx1):
+            tiles = count // P
+            store_result("1_%d" % first, HALF_TILES + first // P, tiles, readout(hnew_mx, tiles))

@@ -44,6 +44,10 @@ def lanes_of_block(u):
     return slice(PAIR * u, PAIR * (u + 1))
 
 
+def node_slices(tiles):
+    return [slice(a * P, (a + tiles) * P) for a in range(0, HALF_TILES, tiles)]
+
+
 def lanes_range(u):
     return range(PAIR * u, PAIR * (u + 1))
 
@@ -254,26 +258,19 @@ def tile_gatedgraphconvolution_pb_kernel(
                 op1=ALU.add,
             )
 
-        def sigmoid_z(z, sums, u):
+        def sigmoid_z(z, sums, nodes):
             nc.scalar.activation(
-                out=z[:, u, :, :],
-                in_=sums[:, lanes_of_block(u), :].rearrange("q e n -> q n e"),
-                func=ACT.Sigmoid,
+                out=z[:, nodes, :], in_=sums[:, :, nodes].rearrange("q t n -> q n t"), func=ACT.Sigmoid
             )
 
         def sigmoid_r(sums, t):
             nc.scalar.activation(out=sums[:, t, :], in_=sums[:, t, :], func=ACT.Sigmoid)
 
-        def keep_state(kept, z, h_lanes, u):
-            h_pairs = h_lanes.rearrange("q (n u e) -> q u n e", u=BLOCKS, e=PAIR)
-            for part in range(PAIR):
-                nodes = slice(part * HALF // PAIR, (part + 1) * HALF // PAIR)
-                nc.gpsimd.tensor_tensor(
-                    out=kept[:, u, nodes, :],
-                    in0=z[:, u, nodes, :],
-                    in1=h_pairs[:, u, nodes, :],
-                    op=ALU.mult,
-                )
+        def keep_state(kept, z, h_lanes, nodes):
+            h_by_node = h_lanes.rearrange("q (n t) -> q n t", t=LANES)
+            nc.gpsimd.tensor_tensor(
+                out=kept[:, nodes, :], in0=z[:, nodes, :], in1=h_by_node[:, nodes, :], op=ALU.mult
+            )
 
         def reset_product(products, t, gh_lanes, r, first, count):
             nc.vector.scalar_tensor_tensor(
@@ -285,37 +282,28 @@ def tile_gatedgraphconvolution_pb_kernel(
                 op1=ALU.mult,
             )
 
-        def candidate_sum(cand, products, u, x_bank, first, count):
+        def candidate_sum(sums, products, u, x_bank, first, count):
             nc.vector.tensor_tensor(
-                out=cand[:, u, :, :],
+                out=sums[:, u, :, :],
                 in0=products[:, lanes_of_block(u), :].rearrange("q e n -> q n e"),
                 in1=pairs_of_words(x_bank[:, first : first + count]),
                 op=ALU.add,
             )
 
-        def tanh_in_place(cand, u):
-            nc.scalar.activation(out=cand[:, u, :, :], in_=cand[:, u, :, :], func=ACT.Tanh)
-
-        def minus_new(product, z, cand, u, first, count):
-            nc.vector.scalar_tensor_tensor(
-                out=product[:, u, :, :],
-                in0=z[:, u, first : first + count, :],
-                scalar=1.0,
-                in1=cand[:, u, :, :],
-                op0=ALU.subtract,
-                op1=ALU.mult,
+        def candidate(cand, sums):
+            nc.scalar.activation(
+                out=cand.rearrange("q n (u e) -> q n u e", u=BLOCKS),
+                in_=sums.rearrange("q u n e -> q n u e"),
+                func=ACT.Tanh,
             )
 
-        def by_node(paired):
-            return paired.rearrange("q u n e -> q n u e")
+        def minus_new(cand, z):
+            nc.vector.scalar_tensor_tensor(
+                out=cand, in0=z, scalar=1.0, in1=cand, op0=ALU.subtract, op1=ALU.mult
+            )
 
         def new_state(engine, hnew, kept, product):
-            engine.tensor_tensor(
-                out=hnew.rearrange("q n (u e) -> q n u e", u=BLOCKS),
-                in0=by_node(kept),
-                in1=by_node(product),
-                op=ALU.subtract,
-            )
+            engine.tensor_tensor(out=hnew, in0=kept, in1=product, op=ALU.subtract)
 
         def quantise_new_state(name, hnew, count):
             codes = halves.tile([P, count], U32, name="hnew_codes" + name, align_bytes=64)
@@ -358,10 +346,10 @@ def tile_gatedgraphconvolution_pb_kernel(
         r_sums = []
         kept = []
         for half in range(HALVES):
-            z.append(halves.tile([P, BLOCKS, HALF, PAIR], F32, name="z%d" % half))
+            z.append(halves.tile([P, HALF, LANES], F32, name="z%d" % half))
             z_sums.append(halves.tile([P, LANES, HALF], F32, name="z_sums%d" % half))
             r_sums.append(halves.tile([P, LANES, HALF], F32, name="r_sums%d" % half))
-            kept.append(halves.tile([P, BLOCKS, HALF, PAIR], F32, name="kept%d" % half))
+            kept.append(halves.tile([P, HALF, LANES], F32, name="kept%d" % half))
 
         h_banks0 = transposed_h(0)
 
@@ -388,9 +376,10 @@ def tile_gatedgraphconvolution_pb_kernel(
         quantise_u(R)
         add_gate_sum(z_sums[0], Z, LANES - 1, gh, x_words)
         x_words = words_in_sbuf(0, R, transposed_gx_blocks(0, R))
-        for u in range(BLOCKS):
-            sigmoid_z(z[0], z_sums[0], u)
-            keep_state(kept[0], z[0], h_lanes0, u)
+        for nodes in node_slices(READ_TILES):
+            sigmoid_z(z[0], z_sums[0], nodes)
+        for nodes in node_slices(1):
+            keep_state(kept[0], z[0], h_lanes0, nodes)
 
         gh = gh_banks(h_mx0, R)
         for t in range(LANES):
@@ -402,36 +391,35 @@ def tile_gatedgraphconvolution_pb_kernel(
         gh = gh_banks(h_mx0, CAND)
         h_lanes1 = h_in_sbuf(1, transposed_h(1))
         products0 = halves.tile([P, LANES, HALF], F32)
-        cand0 = halves.tile([P, BLOCKS, HALF, PAIR], F32)
+        cand_sums0 = halves.tile([P, BLOCKS, HALF, PAIR], F32)
         for t in lanes_range(0):
             reset_product(products0, t, gh, r_sums[0], 0, HALF)
-        candidate_sum(cand0, products0, 0, x_banks[0], 0, HALF)
-        tanh_in_place(cand0, 0)
+        candidate_sum(cand_sums0, products0, 0, x_banks[0], 0, HALF)
         for t in lanes_range(1):
             reset_product(products0, t, gh, r_sums[0], 0, HALF)
         h_mx1 = quantise_h(1, h_lanes1)
-        candidate_sum(cand0, products0, 1, x_banks[1], 0, HALF)
+        candidate_sum(cand_sums0, products0, 1, x_banks[1], 0, HALF)
         x_words = words_in_sbuf(1, Z, transposed_gx_blocks(1, Z))
-        tanh_in_place(cand0, 1)
+        cand0 = halves.tile([P, HALF, LANES], F32)
+        for nodes in node_slices(READ_TILES):
+            candidate(cand0[:, nodes, :], cand_sums0[:, :, nodes, :])
 
         gh = gh_banks(h_mx1, Z)
         for t in lanes_range(0):
             add_gate_sum(z_sums[1], Z, t, gh, x_words)
-        product0 = halves.tile([P, BLOCKS, HALF, PAIR], F32)
-        for u in range(BLOCKS):
-            minus_new(product0, z[0], cand0, u, 0, HALF)
+        for nodes in node_slices(READ_TILES):
+            minus_new(cand0[:, nodes, :], z[0][:, nodes, :])
         for t in lanes_range(1):
             add_gate_sum(z_sums[1], Z, t, gh, x_words)
         x_words = words_in_sbuf(1, R, transposed_gx_blocks(1, R))
-        for u in range(BLOCKS):
-            sigmoid_z(z[1], z_sums[1], u)
+        for nodes in node_slices(READ_TILES):
+            sigmoid_z(z[1], z_sums[1], nodes)
 
         hnew0 = halves.tile([P, HALF, LANES], BF16, align_bytes=64)
-        for a in range(HALF_TILES):
-            nodes = slice(a * P, (a + 1) * P)
-            new_state(nc.gpsimd, hnew0[:, nodes, :], kept[0][:, :, nodes, :], product0[:, :, nodes, :])
-        for u in range(BLOCKS):
-            keep_state(kept[1], z[1], h_lanes1, u)
+        for nodes in node_slices(1):
+            new_state(nc.gpsimd, hnew0[:, nodes, :], kept[0][:, nodes, :], cand0[:, nodes, :])
+        for nodes in node_slices(1):
+            keep_state(kept[1], z[1], h_lanes1, nodes)
 
         gh = gh_banks(h_mx1, R)
         for t in range(LANES):
@@ -445,30 +433,29 @@ def tile_gatedgraphconvolution_pb_kernel(
         for count in LAST_SLICES:
             gh = gh_banks(h_mx1, CAND, first, count)
             products = halves.tile([P, LANES, count], F32, name="products1_%d" % first)
-            cand = halves.tile([P, BLOCKS, count, PAIR], F32, name="cand1_%d" % first)
+            cand_sums = halves.tile([P, BLOCKS, count, PAIR], F32, name="cand_sums1_%d" % first)
+            cand = halves.tile([P, count, LANES], F32, name="cand1_%d" % first)
             for u in range(BLOCKS):
                 for t in lanes_range(u):
                     reset_product(products, t, gh, r_sums[1], first, count)
-                candidate_sum(cand, products, u, x_banks[u], first, count)
-                tanh_in_place(cand, u)
+                candidate_sum(cand_sums, products, u, x_banks[u], first, count)
+            candidate(cand[:], cand_sums[:])
             slices.append((first, count, cand))
             first += count
 
         quantise_w()
         half0_banks = []
-        for s in range(HALF_TILES // READ_TILES):
-            nodes = slice(s * READ_TILES * P, (s + 1) * READ_TILES * P)
+        for s, nodes in enumerate(node_slices(READ_TILES)):
             hnew_mx = quantise_new_state("0_%d" % s, hnew0[:, nodes, :], READ_TILES * P)
             half0_banks.append(readout(hnew_mx, READ_TILES))
         store_result("0_0", 0, READ_TILES, half0_banks[0])
 
         hnew_mx1 = []
         for first, count, cand in slices:
-            product = halves.tile([P, BLOCKS, count, PAIR], F32, name="product1_%d" % first)
+            nodes = slice(first, first + count)
             hnew = halves.tile([P, count, LANES], BF16, name="hnew1_%d" % first, align_bytes=64)
-            for u in range(BLOCKS):
-                minus_new(product, z[1], cand, u, first, count)
-            new_state(nc.vector, hnew[:], kept[1][:, :, first : first + count, :], product[:])
+            minus_new(cand[:], z[1][:, nodes, :])
+            new_state(nc.vector, hnew[:], kept[1][:, nodes, :], cand[:])
             hnew_mx1.append(quantise_new_state("1_%d" % first, hnew[:], count))
             if first == 0:
                 store_result("0_1", READ_TILES, READ_TILES, half0_banks[1])

@@ -27,7 +27,8 @@ HALVES = 2
 HALF_TILES = NODE_TILES // HALVES
 HALF = HALF_TILES * P
 READ_TILES = 2
-LAST_SLICES = (256, 256)
+SLICE = READ_TILES * P
+SLICES = HALF // SLICE
 
 FLOPS = 2 * NODES * CHANNELS * (GATES * CHANNELS + OUTPUTS)
 
@@ -36,20 +37,12 @@ def lane_of_words(words, e):
     return words.bitcast(BF16).rearrange("p (n e) -> p n e", e=PAIR)[:, :, e]
 
 
-def pairs_of_words(words):
-    return words.bitcast(BF16).rearrange("p (n e) -> p n e", e=PAIR)
-
-
 def lanes_of_block(u):
     return slice(PAIR * u, PAIR * (u + 1))
 
 
-def node_slices(tiles):
-    return [slice(a * P, (a + tiles) * P) for a in range(0, HALF_TILES, tiles)]
-
-
-def lanes_range(u):
-    return range(PAIR * u, PAIR * (u + 1))
+def slice_nodes(s):
+    return slice(s * SLICE, (s + 1) * SLICE)
 
 
 def tile_gatedgraphconvolution_pb_kernel(
@@ -65,9 +58,9 @@ def tile_gatedgraphconvolution_pb_kernel(
         inputs = ctx.enter_context(tc.tile_pool(name="inputs", bufs=1))
         weights = ctx.enter_context(tc.tile_pool(name="weights", bufs=1))
         halves = ctx.enter_context(tc.tile_pool(name="halves", bufs=1))
+        work = ctx.enter_context(tc.tile_pool(name="work", bufs=HALVES * SLICES))
         psum_gh = ctx.enter_context(tc.psum_pool(name="psum_gh", bufs=3))
-        psum_words = ctx.enter_context(tc.psum_pool(name="psum_words", bufs=3))
-        psum_pairs = ctx.enter_context(tc.psum_pool(name="psum_pairs", bufs=2))
+        psum_turns = ctx.enter_context(tc.psum_pool(name="psum_turns", bufs=5))
         ctx.enter_context(tc.manual_schedule())
 
         h_sb = []
@@ -108,12 +101,13 @@ def tile_gatedgraphconvolution_pb_kernel(
             nc.sync.dma_start(out=gx_sb[half][gate][:], in_=gx_rows[:, tiles, cols])
 
         load_h(0)
+        load_u(Z)
         nc.vector.memset(bias_rows[:], 0.0)
-        nc.sync.dma_start(
-            out=bias_rows[0 : GATES * BLOCKS, :],
-            in_=gru_b_h.rearrange("(r c) -> r c", c=PAIR * P),
-        )
-        for gate in range(GATES):
+        bias_source = gru_b_h.rearrange("(r c) -> r c", c=PAIR * P)
+        for rows in (slice(0, 4), slice(4, 6)):
+            nc.sync.dma_start(out=bias_rows[rows, :], in_=bias_source[rows, :])
+        load_gx(0, Z)
+        for gate in (R, CAND):
             load_u(gate)
             load_gx(0, gate)
         load_h(1)
@@ -173,7 +167,7 @@ def tile_gatedgraphconvolution_pb_kernel(
             )
 
         def transposed_gx(half, gate, u):
-            bank = psum_words.tile([P, HALF], F32, tag="words")
+            bank = psum_turns.tile([P, HALF], F32, tag="turn")
             for a in range(HALF_TILES):
                 nc.tensor.transpose(
                     bank[:, a * P : (a + 1) * P],
@@ -197,7 +191,7 @@ def tile_gatedgraphconvolution_pb_kernel(
         def transposed_h(half):
             banks = []
             for s in range(HALF_TILES // PAIR):
-                bank = psum_pairs.tile([P, BLOCKS, PAIR * P], F32, tag="pair")
+                bank = psum_turns.tile([P, BLOCKS, PAIR * P], F32, tag="turn")
                 for u in range(BLOCKS):
                     for j in range(PAIR):
                         nc.tensor.transpose(
@@ -223,7 +217,7 @@ def tile_gatedgraphconvolution_pb_kernel(
             nc.vector.quantize_mx(out=h_codes[:].bitcast(FP8X4), scales=h_scales[:], in_=h_lanes)
             return h_codes, h_scales
 
-        def gh_banks(h_mx, gate, first=0, count=HALF):
+        def gh_lanes(h_mx, gate, first=0, count=HALF):
             h_codes, h_scales = h_mx
             nodes = slice(first, first + count)
             in_bank = HALF // count
@@ -248,10 +242,10 @@ def tile_gatedgraphconvolution_pb_kernel(
         def bias_of(gate, t):
             return gate_bias[:, gate * LANES + t : gate * LANES + t + 1]
 
-        def add_gate_sum(sums, gate, t, gh_lanes, x_words):
+        def add_gate_sum(sums, gate, t, gh, x_words):
             nc.vector.scalar_tensor_tensor(
                 out=sums[:, t, :],
-                in0=gh_lanes[t],
+                in0=gh[t],
                 scalar=bias_of(gate, t),
                 in1=lane_of_words(x_words[:, t // PAIR, :], t % PAIR),
                 op0=ALU.add,
@@ -266,36 +260,42 @@ def tile_gatedgraphconvolution_pb_kernel(
         def sigmoid_r(sums, t):
             nc.scalar.activation(out=sums[:, t, :], in_=sums[:, t, :], func=ACT.Sigmoid)
 
-        def keep_state(kept, z, h_lanes, nodes):
+        def node_tiles(s):
+            tiles = []
+            for a in range(s * READ_TILES, (s + 1) * READ_TILES):
+                tiles.append(slice(a * P, (a + 1) * P))
+            return tiles
+
+        def keep_state(engine, kept, z, h_lanes, nodes):
             h_by_node = h_lanes.rearrange("q (n t) -> q n t", t=LANES)
-            nc.gpsimd.tensor_tensor(
+            engine.tensor_tensor(
                 out=kept[:, nodes, :], in0=z[:, nodes, :], in1=h_by_node[:, nodes, :], op=ALU.mult
             )
 
-        def reset_product(products, t, gh_lanes, r, first, count):
+        def keep_on_gpsimd(kept, z, h_lanes, s):
+            for nodes in node_tiles(s):
+                keep_state(nc.gpsimd, kept, z, h_lanes, nodes)
+
+        def reset_product(products, t, gh, r, s):
             nc.vector.scalar_tensor_tensor(
                 out=products[:, t, :],
-                in0=gh_lanes[t],
+                in0=gh[t],
                 scalar=bias_of(CAND, t),
-                in1=r[:, t, first : first + count],
+                in1=r[:, t, slice_nodes(s)],
                 op0=ALU.add,
                 op1=ALU.mult,
             )
 
-        def candidate_sum(sums, products, u, x_bank, first, count):
+        def candidate_sum(products, t, x_bank, s):
             nc.vector.tensor_tensor(
-                out=sums[:, u, :, :],
-                in0=products[:, lanes_of_block(u), :].rearrange("q e n -> q n e"),
-                in1=pairs_of_words(x_bank[:, first : first + count]),
+                out=products[:, t, :],
+                in0=products[:, t, :],
+                in1=lane_of_words(x_bank[:, slice_nodes(s)], t % PAIR),
                 op=ALU.add,
             )
 
         def candidate(cand, sums):
-            nc.scalar.activation(
-                out=cand.rearrange("q n (u e) -> q n u e", u=BLOCKS),
-                in_=sums.rearrange("q u n e -> q n u e"),
-                func=ACT.Tanh,
-            )
+            nc.scalar.activation(out=cand, in_=sums.rearrange("q t n -> q n t"), func=ACT.Tanh)
 
         def minus_new(cand, z):
             nc.vector.scalar_tensor_tensor(
@@ -305,9 +305,9 @@ def tile_gatedgraphconvolution_pb_kernel(
         def new_state(engine, hnew, kept, product):
             engine.tensor_tensor(out=hnew, in0=kept, in1=product, op=ALU.subtract)
 
-        def quantise_new_state(name, hnew, count):
-            codes = halves.tile([P, count], U32, name="hnew_codes" + name, align_bytes=64)
-            scales = halves.tile([P, count], U8, name="hnew_scales" + name, align_bytes=64)
+        def quantise_new_state(hnew):
+            codes = work.tile([P, SLICE], U32, tag="hnew_codes", align_bytes=64)
+            scales = work.tile([P, SLICE], U8, tag="hnew_scales", align_bytes=64)
             nc.vector.quantize_mx(
                 out=codes[:].bitcast(FP8X4),
                 scales=scales[:],
@@ -315,10 +315,10 @@ def tile_gatedgraphconvolution_pb_kernel(
             )
             return codes, scales
 
-        def readout(hnew_mx, tiles):
+        def readout(hnew_mx):
             codes, scales = hnew_mx
-            bank = psum_pairs.tile([P, READ_TILES, OUTPUTS], F32, tag="pair")
-            for j in range(tiles):
+            bank = psum_turns.tile([P, READ_TILES, OUTPUTS], F32, tag="turn")
+            for j in range(READ_TILES):
                 nodes = slice(j * P, (j + 1) * P)
                 nc.tensor.matmul_mx(
                     out=bank[:, j, :],
@@ -331,134 +331,140 @@ def tile_gatedgraphconvolution_pb_kernel(
                 )
             return bank
 
-        def store_result(name, first_tile, tiles, bank):
-            result = halves.tile([P, tiles, OUTPUTS], F32, name="result" + name)
+        def store_result(half, s, bank):
+            result = work.tile([P, READ_TILES, OUTPUTS], F32, tag="result")
             nc.vector.tensor_tensor(
                 out=result[:],
-                in0=bank[:, 0:tiles, :],
-                in1=dense_bias[:].unsqueeze(1).to_broadcast([P, tiles, OUTPUTS]),
+                in0=bank[:],
+                in1=dense_bias[:].unsqueeze(1).to_broadcast([P, READ_TILES, OUTPUTS]),
                 op=ALU.add,
             )
-            nc.sync.dma_start(out=out_rows[:, first_tile : first_tile + tiles, :], in_=result[:])
+            first_tile = half * HALF_TILES + s * READ_TILES
+            nc.sync.dma_start(out=out_rows[:, first_tile : first_tile + READ_TILES, :], in_=result[:])
 
         z = []
         z_sums = []
         r_sums = []
         kept = []
+        hnew = []
+        cand = []
         for half in range(HALVES):
             z.append(halves.tile([P, HALF, LANES], F32, name="z%d" % half))
             z_sums.append(halves.tile([P, LANES, HALF], F32, name="z_sums%d" % half))
             r_sums.append(halves.tile([P, LANES, HALF], F32, name="r_sums%d" % half))
             kept.append(halves.tile([P, HALF, LANES], F32, name="kept%d" % half))
+            hnew.append(halves.tile([P, HALF, LANES], BF16, name="hnew%d" % half, align_bytes=64))
+            cand.append(halves.tile([P, HALF, LANES], F32, name="cand%d" % half))
+
+        def candidate_slice(half, s, gh, x_banks, between):
+            products = work.tile([P, LANES, SLICE], F32, tag="products")
+            for t in range(LANES):
+                reset_product(products, t, gh, r_sums[half], s)
+            between()
+            for t in range(LANES):
+                candidate_sum(products, t, x_banks[t // PAIR], s)
+            candidate(cand[half][:, slice_nodes(s), :], products[:])
+
+        def minus_new_slice(half, s):
+            minus_new(cand[half][:, slice_nodes(s), :], z[half][:, slice_nodes(s), :])
+
+        def new_state_on_vector(half, s):
+            nodes = slice_nodes(s)
+            new_state(nc.vector, hnew[half][:, nodes, :], kept[half][:, nodes, :], cand[half][:, nodes, :])
+
+        def new_state_on_gpsimd(half, s):
+            for nodes in node_tiles(s):
+                new_state(
+                    nc.gpsimd, hnew[half][:, nodes, :], kept[half][:, nodes, :], cand[half][:, nodes, :]
+                )
+
+        def read_out(half, s):
+            return readout(quantise_new_state(hnew[half][:, slice_nodes(s), :]))
+
+        def nothing():
+            pass
 
         h_banks0 = transposed_h(0)
-
-        bias_bank = psum_words.tile([P, HALF], F32, tag="words")
+        bias_bank = psum_turns.tile([P, HALF], F32, tag="turn")
         nc.tensor.transpose(bias_bank[:, 0:P], bias_rows[:].bitcast(F32), ident[:])
         gate_bias = const.tile([P, GATES * LANES], F32)
-
         h_lanes0 = h_in_sbuf(0, h_banks0)
-        for u in range(BLOCKS):
-            group_u(Z, u, nc.vector.tensor_copy)
-        nc.vector.tensor_copy(out=gate_bias[:], in_=bias_bank[:, 0 : GATES * BLOCKS].bitcast(BF16))
+        group_u(Z, 0, nc.vector.tensor_copy)
         h_mx0 = quantise_h(0, h_lanes0)
         quantise_u(Z, 0, CHANNELS // 2)
+        group_u(Z, 1, nc.vector.tensor_copy)
+        nc.vector.tensor_copy(out=gate_bias[:], in_=bias_bank[:, 0 : GATES * BLOCKS].bitcast(BF16))
         quantise_u(Z, CHANNELS // 2, CHANNELS // 2)
         x_words = words_in_sbuf(0, Z, transposed_gx_blocks(0, Z))
         group_u(R, 0, nc.scalar.copy)
         group_u(R, 1, gpsimd_copy)
+
+        gh = gh_lanes(h_mx0, Z)
+        for t in range(LANES):
+            add_gate_sum(z_sums[0], Z, t, gh, x_words)
+            if t == LANES - 2:
+                quantise_u(R)
+        x_words = words_in_sbuf(0, R, transposed_gx_blocks(0, R))
         for u in range(BLOCKS):
             group_u(CAND, u, gpsimd_copy)
 
-        gh = gh_banks(h_mx0, Z)
-        for t in range(LANES - 1):
-            add_gate_sum(z_sums[0], Z, t, gh, x_words)
-        quantise_u(R)
-        add_gate_sum(z_sums[0], Z, LANES - 1, gh, x_words)
-        x_words = words_in_sbuf(0, R, transposed_gx_blocks(0, R))
-        for nodes in node_slices(READ_TILES):
-            sigmoid_z(z[0], z_sums[0], nodes)
-        for nodes in node_slices(1):
-            keep_state(kept[0], z[0], h_lanes0, nodes)
-
-        gh = gh_banks(h_mx0, R)
+        gh = gh_lanes(h_mx0, R)
         for t in range(LANES):
+            if t == LANES - 1:
+                quantise_u(CAND)
             add_gate_sum(r_sums[0], R, t, gh, x_words)
             sigmoid_r(r_sums[0], t)
-        quantise_u(CAND)
+            if t == 0:
+                sigmoid_z(z[0], z_sums[0], slice_nodes(0))
+                keep_on_gpsimd(kept[0], z[0], h_lanes0, 0)
 
-        x_banks = transposed_gx_blocks(0, CAND)
-        gh = gh_banks(h_mx0, CAND)
         h_lanes1 = h_in_sbuf(1, transposed_h(1))
-        products0 = halves.tile([P, LANES, HALF], F32)
-        cand_sums0 = halves.tile([P, BLOCKS, HALF, PAIR], F32)
-        for t in lanes_range(0):
-            reset_product(products0, t, gh, r_sums[0], 0, HALF)
-        candidate_sum(cand_sums0, products0, 0, x_banks[0], 0, HALF)
-        for t in lanes_range(1):
-            reset_product(products0, t, gh, r_sums[0], 0, HALF)
+        sigmoid_z(z[0], z_sums[0], slice_nodes(1))
+        keep_on_gpsimd(kept[0], z[0], h_lanes0, 1)
+        x_banks = transposed_gx_blocks(0, CAND)
+        gh = gh_lanes(h_mx0, CAND, 0, SLICE)
+        candidate_slice(0, 0, gh, x_banks, nothing)
+        gh = gh_lanes(h_mx0, CAND, SLICE, SLICE)
         h_mx1 = quantise_h(1, h_lanes1)
-        candidate_sum(cand_sums0, products0, 1, x_banks[1], 0, HALF)
         x_words = words_in_sbuf(1, Z, transposed_gx_blocks(1, Z))
-        cand0 = halves.tile([P, HALF, LANES], F32)
-        for nodes in node_slices(READ_TILES):
-            candidate(cand0[:, nodes, :], cand_sums0[:, :, nodes, :])
+        candidate_slice(0, 1, gh, x_banks, nothing)
 
-        gh = gh_banks(h_mx1, Z)
-        for t in lanes_range(0):
+        gh = gh_lanes(h_mx1, Z)
+        for t in range(LANES):
             add_gate_sum(z_sums[1], Z, t, gh, x_words)
-        for nodes in node_slices(READ_TILES):
-            minus_new(cand0[:, nodes, :], z[0][:, nodes, :])
-        for t in lanes_range(1):
-            add_gate_sum(z_sums[1], Z, t, gh, x_words)
+            if t == 1:
+                for s in range(SLICES):
+                    minus_new_slice(0, s)
         x_words = words_in_sbuf(1, R, transposed_gx_blocks(1, R))
-        for nodes in node_slices(READ_TILES):
-            sigmoid_z(z[1], z_sums[1], nodes)
+        sigmoid_z(z[1], z_sums[1], slice_nodes(0))
 
-        hnew0 = halves.tile([P, HALF, LANES], BF16, align_bytes=64)
-        for nodes in node_slices(1):
-            new_state(nc.gpsimd, hnew0[:, nodes, :], kept[0][:, nodes, :], cand0[:, nodes, :])
-        for nodes in node_slices(1):
-            keep_state(kept[1], z[1], h_lanes1, nodes)
+        for s in range(SLICES):
+            new_state_on_gpsimd(0, s)
+        keep_on_gpsimd(kept[1], z[1], h_lanes1, 0)
 
-        gh = gh_banks(h_mx1, R)
+        gh = gh_lanes(h_mx1, R)
         for t in range(LANES):
             add_gate_sum(r_sums[1], R, t, gh, x_words)
             sigmoid_r(r_sums[1], t)
+        sigmoid_z(z[1], z_sums[1], slice_nodes(1))
+        keep_on_gpsimd(kept[1], z[1], h_lanes1, 1)
         group_w()
 
         x_banks = transposed_gx_blocks(1, CAND)
-        slices = []
-        first = 0
-        for count in LAST_SLICES:
-            gh = gh_banks(h_mx1, CAND, first, count)
-            products = halves.tile([P, LANES, count], F32, name="products1_%d" % first)
-            cand_sums = halves.tile([P, BLOCKS, count, PAIR], F32, name="cand_sums1_%d" % first)
-            cand = halves.tile([P, count, LANES], F32, name="cand1_%d" % first)
-            for u in range(BLOCKS):
-                for t in lanes_range(u):
-                    reset_product(products, t, gh, r_sums[1], first, count)
-                candidate_sum(cand_sums, products, u, x_banks[u], first, count)
-            candidate(cand[:], cand_sums[:])
-            slices.append((first, count, cand))
-            first += count
+        for s in range(SLICES):
+            gh = gh_lanes(h_mx1, CAND, s * SLICE, SLICE)
+            candidate_slice(1, s, gh, x_banks, nothing)
 
         quantise_w()
-        half0_banks = []
-        for s, nodes in enumerate(node_slices(READ_TILES)):
-            hnew_mx = quantise_new_state("0_%d" % s, hnew0[:, nodes, :], READ_TILES * P)
-            half0_banks.append(readout(hnew_mx, READ_TILES))
-        store_result("0_0", 0, READ_TILES, half0_banks[0])
-
-        hnew_mx1 = []
-        for first, count, cand in slices:
-            nodes = slice(first, first + count)
-            hnew = halves.tile([P, count, LANES], BF16, name="hnew1_%d" % first, align_bytes=64)
-            minus_new(cand[:], z[1][:, nodes, :])
-            new_state(nc.vector, hnew[:], kept[1][:, nodes, :], cand[:])
-            hnew_mx1.append(quantise_new_state("1_%d" % first, hnew[:], count))
-            if first == 0:
-                store_result("0_1", READ_TILES, READ_TILES, half0_banks[1])
-        for (first, count, cand), hnew_mx in zip(slices, hnew_mx1):
-            tiles = count // P
-            store_result("1_%d" % first, HALF_TILES + first // P, tiles, readout(hnew_mx, tiles))
+        banks0 = []
+        for s in range(SLICES):
+            banks0.append(read_out(0, s))
+        minus_new_slice(1, 0)
+        store_result(0, 0, banks0[0])
+        new_state_on_vector(1, 0)
+        minus_new_slice(1, 1)
+        bank = read_out(1, 0)
+        store_result(0, 1, banks0[1])
+        new_state_on_vector(1, 1)
+        store_result(1, 0, bank)
+        store_result(1, 1, read_out(1, 1))

@@ -217,27 +217,26 @@ def tile_gatedgraphconvolution_pb_kernel(
             nc.vector.quantize_mx(out=h_codes[:].bitcast(FP8X4), scales=h_scales[:], in_=h_lanes)
             return h_codes, h_scales
 
-        def gh_lanes(h_mx, gate, first=0, count=HALF):
+        def gh_bank(h_mx, gate, t):
             h_codes, h_scales = h_mx
-            nodes = slice(first, first + count)
-            in_bank = HALF // count
-            lanes = []
+            bank = psum_gh.tile([P, HALF], F32, tag="gh")
+            positions = slice(t * P, (t + 1) * P)
+            nc.tensor.matmul_mx(
+                out=bank[:],
+                lhsT=u_codes[gate][:, positions].bitcast(FP8X4),
+                lhsT_scale=u_scales[gate][:, positions],
+                rhs=h_codes[:].bitcast(FP8X4),
+                rhs_scale=h_scales[:],
+                start=True,
+                stop=True,
+            )
+            return bank
+
+        def gh_banks(h_mx, gate):
+            banks = []
             for t in range(LANES):
-                if t % in_bank == 0:
-                    bank = psum_gh.tile([P, HALF], F32, tag="gh")
-                place = t % in_bank * count
-                positions = slice(t * P, (t + 1) * P)
-                nc.tensor.matmul_mx(
-                    out=bank[:, place : place + count],
-                    lhsT=u_codes[gate][:, positions].bitcast(FP8X4),
-                    lhsT_scale=u_scales[gate][:, positions],
-                    rhs=h_codes[:, nodes].bitcast(FP8X4),
-                    rhs_scale=h_scales[:, nodes],
-                    start=True,
-                    stop=True,
-                )
-                lanes.append(bank[:, place : place + count])
-            return lanes
+                banks.append(gh_bank(h_mx, gate, t))
+            return banks
 
         def bias_of(gate, t):
             return gate_bias[:, gate * LANES + t : gate * LANES + t + 1]
@@ -245,7 +244,7 @@ def tile_gatedgraphconvolution_pb_kernel(
         def add_gate_sum(sums, gate, t, gh, x_words):
             nc.vector.scalar_tensor_tensor(
                 out=sums[:, t, :],
-                in0=gh[t],
+                in0=gh[t][:],
                 scalar=bias_of(gate, t),
                 in1=lane_of_words(x_words[:, t // PAIR, :], t % PAIR),
                 op0=ALU.add,
@@ -276,21 +275,21 @@ def tile_gatedgraphconvolution_pb_kernel(
             for nodes in node_tiles(s):
                 keep_state(nc.gpsimd, kept, z, h_lanes, nodes)
 
-        def reset_product(products, t, gh, r, s):
+        def reset_product(products, t, gh, r):
             nc.vector.scalar_tensor_tensor(
                 out=products[:, t, :],
-                in0=gh[t],
+                in0=gh[t][:],
                 scalar=bias_of(CAND, t),
-                in1=r[:, t, slice_nodes(s)],
+                in1=r[:, t, :],
                 op0=ALU.add,
                 op1=ALU.mult,
             )
 
-        def candidate_sum(products, t, x_bank, s):
+        def candidate_sum(products, t, x_bank):
             nc.vector.tensor_tensor(
                 out=products[:, t, :],
                 in0=products[:, t, :],
-                in1=lane_of_words(x_bank[:, slice_nodes(s)], t % PAIR),
+                in1=lane_of_words(x_bank[:], t % PAIR),
                 op=ALU.add,
             )
 
@@ -356,15 +355,6 @@ def tile_gatedgraphconvolution_pb_kernel(
             hnew.append(halves.tile([P, HALF, LANES], BF16, name="hnew%d" % half, align_bytes=64))
             cand.append(halves.tile([P, HALF, LANES], F32, name="cand%d" % half))
 
-        def candidate_slice(half, s, gh, x_banks, between):
-            products = work.tile([P, LANES, SLICE], F32, tag="products")
-            for t in range(LANES):
-                reset_product(products, t, gh, r_sums[half], s)
-            between()
-            for t in range(LANES):
-                candidate_sum(products, t, x_banks[t // PAIR], s)
-            candidate(cand[half][:, slice_nodes(s), :], products[:])
-
         def minus_new_slice(half, s):
             minus_new(cand[half][:, slice_nodes(s), :], z[half][:, slice_nodes(s), :])
 
@@ -381,9 +371,6 @@ def tile_gatedgraphconvolution_pb_kernel(
         def read_out(half, s):
             return readout(quantise_new_state(hnew[half][:, slice_nodes(s), :]))
 
-        def nothing():
-            pass
-
         h_banks0 = transposed_h(0)
         bias_bank = psum_turns.tile([P, HALF], F32, tag="turn")
         nc.tensor.transpose(bias_bank[:, 0:P], bias_rows[:].bitcast(F32), ident[:])
@@ -399,7 +386,7 @@ def tile_gatedgraphconvolution_pb_kernel(
         group_u(R, 0, nc.scalar.copy)
         group_u(R, 1, gpsimd_copy)
 
-        gh = gh_lanes(h_mx0, Z)
+        gh = gh_banks(h_mx0, Z)
         for t in range(LANES):
             add_gate_sum(z_sums[0], Z, t, gh, x_words)
             if t == LANES - 2:
@@ -408,7 +395,7 @@ def tile_gatedgraphconvolution_pb_kernel(
         for u in range(BLOCKS):
             group_u(CAND, u, gpsimd_copy)
 
-        gh = gh_lanes(h_mx0, R)
+        gh = gh_banks(h_mx0, R)
         for t in range(LANES):
             if t == LANES - 1:
                 quantise_u(CAND)
@@ -422,19 +409,22 @@ def tile_gatedgraphconvolution_pb_kernel(
         sigmoid_z(z[0], z_sums[0], slice_nodes(1))
         keep_on_gpsimd(kept[0], z[0], h_lanes0, 1)
         x_banks = transposed_gx_blocks(0, CAND)
-        gh = gh_lanes(h_mx0, CAND, 0, SLICE)
-        candidate_slice(0, 0, gh, x_banks, nothing)
-        gh = gh_lanes(h_mx0, CAND, SLICE, SLICE)
+        gh = gh_banks(h_mx0, CAND)
+        products = halves.tile([P, LANES, HALF], F32, name="products0")
+        for t in range(LANES):
+            reset_product(products, t, gh, r_sums[0])
         h_mx1 = quantise_h(1, h_lanes1)
         x_words = words_in_sbuf(1, Z, transposed_gx_blocks(1, Z))
-        candidate_slice(0, 1, gh, x_banks, nothing)
+        for t in range(LANES):
+            candidate_sum(products, t, x_banks[t // PAIR])
+        for s in range(SLICES):
+            candidate(cand[0][:, slice_nodes(s), :], products[:, :, slice_nodes(s)])
 
-        gh = gh_lanes(h_mx1, Z)
+        gh = gh_banks(h_mx1, Z)
         for t in range(LANES):
             add_gate_sum(z_sums[1], Z, t, gh, x_words)
-            if t == 1:
-                for s in range(SLICES):
-                    minus_new_slice(0, s)
+        for s in range(SLICES):
+            minus_new_slice(0, s)
         x_words = words_in_sbuf(1, R, transposed_gx_blocks(1, R))
         sigmoid_z(z[1], z_sums[1], slice_nodes(0))
 
@@ -442,19 +432,24 @@ def tile_gatedgraphconvolution_pb_kernel(
             new_state_on_gpsimd(0, s)
         keep_on_gpsimd(kept[1], z[1], h_lanes1, 0)
 
-        gh = gh_lanes(h_mx1, R)
+        gh = gh_banks(h_mx1, R)
         for t in range(LANES):
             add_gate_sum(r_sums[1], R, t, gh, x_words)
             sigmoid_r(r_sums[1], t)
         sigmoid_z(z[1], z_sums[1], slice_nodes(1))
-        keep_on_gpsimd(kept[1], z[1], h_lanes1, 1)
         group_w()
 
         x_banks = transposed_gx_blocks(1, CAND)
+        gh = gh_banks(h_mx1, CAND)
+        products = halves.tile([P, LANES, HALF], F32, name="products1")
+        for t in range(LANES):
+            reset_product(products, t, gh, r_sums[1])
+        for t in range(LANES):
+            candidate_sum(products, t, x_banks[t // PAIR])
         for s in range(SLICES):
-            gh = gh_lanes(h_mx1, CAND, s * SLICE, SLICE)
-            candidate_slice(1, s, gh, x_banks, nothing)
+            candidate(cand[1][:, slice_nodes(s), :], products[:, :, slice_nodes(s)])
 
+        keep_state(nc.vector, kept[1], z[1], h_lanes1, slice_nodes(1))
         quantise_w()
         banks0 = []
         for s in range(SLICES):

@@ -251,29 +251,25 @@ def tile_gatedgraphconvolution_pb_kernel(
                 op1=ALU.add,
             )
 
-        def sigmoid_z(z, sums, nodes):
+        def paired_function(out, lanes, u, func):
             nc.scalar.activation(
-                out=z[:, nodes, :], in_=sums[:, :, nodes].rearrange("q t n -> q n t"), func=ACT.Sigmoid
+                out=out[:, u, :, :],
+                in_=lanes[:, lanes_of_block(u), :].rearrange("q e n -> q n e"),
+                func=func,
             )
 
         def sigmoid_r(sums, t):
             nc.scalar.activation(out=sums[:, t, :], in_=sums[:, t, :], func=ACT.Sigmoid)
 
-        def node_tiles(s):
-            tiles = []
-            for a in range(s * READ_TILES, (s + 1) * READ_TILES):
-                tiles.append(slice(a * P, (a + 1) * P))
-            return tiles
-
-        def keep_state(engine, kept, z, h_lanes, nodes):
-            h_by_node = h_lanes.rearrange("q (n t) -> q n t", t=LANES)
+        def keep_state(engine, kept, z, h_lanes, u, nodes):
+            h_pairs = h_lanes.rearrange("q (n u e) -> q u n e", u=BLOCKS, e=PAIR)
             engine.tensor_tensor(
-                out=kept[:, nodes, :], in0=z[:, nodes, :], in1=h_by_node[:, nodes, :], op=ALU.mult
+                out=kept[:, u, nodes, :], in0=z[:, u, nodes, :], in1=h_pairs[:, u, nodes, :], op=ALU.mult
             )
 
-        def keep_on_gpsimd(kept, z, h_lanes, s):
-            for nodes in node_tiles(s):
-                keep_state(nc.gpsimd, kept, z, h_lanes, nodes)
+        def keep_on_gpsimd(kept, z, h_lanes, u):
+            for s in range(SLICES):
+                keep_state(nc.gpsimd, kept, z, h_lanes, u, slice_nodes(s))
 
         def reset_product(products, t, gh, r):
             nc.vector.scalar_tensor_tensor(
@@ -293,16 +289,23 @@ def tile_gatedgraphconvolution_pb_kernel(
                 op=ALU.add,
             )
 
-        def candidate(cand, sums):
-            nc.scalar.activation(out=cand, in_=sums.rearrange("q t n -> q n t"), func=ACT.Tanh)
-
-        def minus_new(cand, z):
+        def minus_new(cand, z, u):
             nc.vector.scalar_tensor_tensor(
-                out=cand, in0=z, scalar=1.0, in1=cand, op0=ALU.subtract, op1=ALU.mult
+                out=cand[:, u, :, :],
+                in0=z[:, u, :, :],
+                scalar=1.0,
+                in1=cand[:, u, :, :],
+                op0=ALU.subtract,
+                op1=ALU.mult,
             )
 
-        def new_state(engine, hnew, kept, product):
-            engine.tensor_tensor(out=hnew, in0=kept, in1=product, op=ALU.subtract)
+        def new_state(engine, hnew, kept, product, nodes):
+            engine.tensor_tensor(
+                out=hnew[:, nodes, :].rearrange("q n (u e) -> q n u e", u=BLOCKS),
+                in0=kept[:, :, nodes, :].rearrange("q u n e -> q n u e"),
+                in1=product[:, :, nodes, :].rearrange("q u n e -> q n u e"),
+                op=ALU.subtract,
+            )
 
         def quantise_new_state(hnew):
             codes = work.tile([P, SLICE], U32, tag="hnew_codes", align_bytes=64)
@@ -348,25 +351,12 @@ def tile_gatedgraphconvolution_pb_kernel(
         hnew = []
         cand = []
         for half in range(HALVES):
-            z.append(halves.tile([P, HALF, LANES], F32, name="z%d" % half))
+            z.append(halves.tile([P, BLOCKS, HALF, PAIR], F32, name="z%d" % half))
             z_sums.append(halves.tile([P, LANES, HALF], F32, name="z_sums%d" % half))
             r_sums.append(halves.tile([P, LANES, HALF], F32, name="r_sums%d" % half))
-            kept.append(halves.tile([P, HALF, LANES], F32, name="kept%d" % half))
+            kept.append(halves.tile([P, BLOCKS, HALF, PAIR], F32, name="kept%d" % half))
             hnew.append(halves.tile([P, HALF, LANES], BF16, name="hnew%d" % half, align_bytes=64))
-            cand.append(halves.tile([P, HALF, LANES], F32, name="cand%d" % half))
-
-        def minus_new_slice(half, s):
-            minus_new(cand[half][:, slice_nodes(s), :], z[half][:, slice_nodes(s), :])
-
-        def new_state_on_vector(half, s):
-            nodes = slice_nodes(s)
-            new_state(nc.vector, hnew[half][:, nodes, :], kept[half][:, nodes, :], cand[half][:, nodes, :])
-
-        def new_state_on_gpsimd(half, s):
-            for nodes in node_tiles(s):
-                new_state(
-                    nc.gpsimd, hnew[half][:, nodes, :], kept[half][:, nodes, :], cand[half][:, nodes, :]
-                )
+            cand.append(halves.tile([P, BLOCKS, HALF, PAIR], F32, name="cand%d" % half))
 
         def read_out(half, s):
             return readout(quantise_new_state(hnew[half][:, slice_nodes(s), :]))
@@ -400,13 +390,13 @@ def tile_gatedgraphconvolution_pb_kernel(
             if t == LANES - 1:
                 quantise_u(CAND)
             add_gate_sum(r_sums[0], R, t, gh, x_words)
-            sigmoid_r(r_sums[0], t)
-            if t == 0:
-                sigmoid_z(z[0], z_sums[0], slice_nodes(0))
+            if t == 1:
+                paired_function(z[0], z_sums[0], 0, ACT.Sigmoid)
                 keep_on_gpsimd(kept[0], z[0], h_lanes0, 0)
+            sigmoid_r(r_sums[0], t)
 
         h_lanes1 = h_in_sbuf(1, transposed_h(1))
-        sigmoid_z(z[0], z_sums[0], slice_nodes(1))
+        paired_function(z[0], z_sums[0], 1, ACT.Sigmoid)
         keep_on_gpsimd(kept[0], z[0], h_lanes0, 1)
         x_banks = transposed_gx_blocks(0, CAND)
         gh = gh_banks(h_mx0, CAND)
@@ -417,26 +407,27 @@ def tile_gatedgraphconvolution_pb_kernel(
         x_words = words_in_sbuf(1, Z, transposed_gx_blocks(1, Z))
         for t in range(LANES):
             candidate_sum(products, t, x_banks[t // PAIR])
-        for s in range(SLICES):
-            candidate(cand[0][:, slice_nodes(s), :], products[:, :, slice_nodes(s)])
+        for u in range(BLOCKS):
+            paired_function(cand[0], products, u, ACT.Tanh)
 
         gh = gh_banks(h_mx1, Z)
         for t in range(LANES):
             add_gate_sum(z_sums[1], Z, t, gh, x_words)
-        for s in range(SLICES):
-            minus_new_slice(0, s)
+            if t == 1:
+                for u in range(BLOCKS):
+                    minus_new(cand[0], z[0], u)
         x_words = words_in_sbuf(1, R, transposed_gx_blocks(1, R))
-        sigmoid_z(z[1], z_sums[1], slice_nodes(0))
+        paired_function(z[1], z_sums[1], 0, ACT.Sigmoid)
 
-        for s in range(SLICES):
-            new_state_on_gpsimd(0, s)
+        for a in range(HALF_TILES):
+            new_state(nc.gpsimd, hnew[0], kept[0], cand[0], slice(a * P, (a + 1) * P))
         keep_on_gpsimd(kept[1], z[1], h_lanes1, 0)
 
         gh = gh_banks(h_mx1, R)
         for t in range(LANES):
             add_gate_sum(r_sums[1], R, t, gh, x_words)
             sigmoid_r(r_sums[1], t)
-        sigmoid_z(z[1], z_sums[1], slice_nodes(1))
+        paired_function(z[1], z_sums[1], 1, ACT.Sigmoid)
         group_w()
 
         x_banks = transposed_gx_blocks(1, CAND)
@@ -446,20 +437,21 @@ def tile_gatedgraphconvolution_pb_kernel(
             reset_product(products, t, gh, r_sums[1])
         for t in range(LANES):
             candidate_sum(products, t, x_banks[t // PAIR])
-        for s in range(SLICES):
-            candidate(cand[1][:, slice_nodes(s), :], products[:, :, slice_nodes(s)])
+        for u in range(BLOCKS):
+            paired_function(cand[1], products, u, ACT.Tanh)
 
-        keep_state(nc.vector, kept[1], z[1], h_lanes1, slice_nodes(1))
+        keep_state(nc.vector, kept[1], z[1], h_lanes1, 1, slice(0, HALF))
         quantise_w()
         banks0 = []
         for s in range(SLICES):
             banks0.append(read_out(0, s))
-        minus_new_slice(1, 0)
+        minus_new(cand[1], z[1], 0)
         store_result(0, 0, banks0[0])
-        new_state_on_vector(1, 0)
-        minus_new_slice(1, 1)
-        bank = read_out(1, 0)
+        minus_new(cand[1], z[1], 1)
         store_result(0, 1, banks0[1])
-        new_state_on_vector(1, 1)
+        new_state(nc.vector, hnew[1], kept[1], cand[1], slice_nodes(0))
+        new_state(nc.vector, hnew[1], kept[1], cand[1], slice_nodes(1))
+        bank = read_out(1, 0)
+        bank_last = read_out(1, 1)
         store_result(1, 0, bank)
-        store_result(1, 1, read_out(1, 1))
+        store_result(1, 1, bank_last)

@@ -60,7 +60,8 @@ def tile_gatedgraphconvolution_pb_kernel(
         halves = ctx.enter_context(tc.tile_pool(name="halves", bufs=1))
         work = ctx.enter_context(tc.tile_pool(name="work", bufs=HALVES * SLICES))
         psum_gh = ctx.enter_context(tc.psum_pool(name="psum_gh", bufs=3))
-        psum_turns = ctx.enter_context(tc.psum_pool(name="psum_turns", bufs=5))
+        psum_turns = ctx.enter_context(tc.psum_pool(name="psum_turns", bufs=4))
+        psum_idle = ctx.enter_context(tc.psum_pool(name="psum_idle", bufs=1))
         ctx.enter_context(tc.manual_schedule())
 
         h_sb = []
@@ -100,6 +101,9 @@ def tile_gatedgraphconvolution_pb_kernel(
             cols = slice(gate * CHANNELS, (gate + 1) * CHANNELS)
             nc.sync.dma_start(out=gx_sb[half][gate][:], in_=gx_rows[:, tiles, cols])
 
+        zeros = const.tile([P, P], F32)
+        warm = const.tile([P, 1], F32)
+        nc.vector.memset(zeros[:], 0.0)
         load_h(0)
         load_u(Z)
         nc.vector.memset(bias_rows[:], 0.0)
@@ -119,9 +123,7 @@ def tile_gatedgraphconvolution_pb_kernel(
         ident = const.tile([P, P], F32)
         make_identity(nc, ident[:])
 
-        warm = const.tile([P, 1], F32)
-        nc.vector.memset(warm[:], 0.0)
-        nc.scalar.activation(out=warm[:], in_=warm[:], func=ACT.Sigmoid)
+        nc.scalar.activation(out=warm[:], in_=zeros[:, 0:1], func=ACT.Sigmoid)
 
         u_grouped = []
         u_codes = []
@@ -237,6 +239,14 @@ def tile_gatedgraphconvolution_pb_kernel(
             for t in range(LANES):
                 banks.append(gh_bank(h_mx, gate, t))
             return banks
+
+        idle_bank = psum_idle.tile([P, HALF], F32)
+
+        def keep_busy(count):
+            for i in range(count):
+                nc.tensor.matmul(
+                    out=idle_bank[:, 0:P], lhsT=zeros[:], rhs=zeros[:], start=True, stop=True
+                )
 
         def bias_of(gate, t):
             return gate_bias[:, gate * LANES + t : gate * LANES + t + 1]
@@ -361,16 +371,19 @@ def tile_gatedgraphconvolution_pb_kernel(
         def read_out(half, s):
             return readout(quantise_new_state(hnew[half][:, slice_nodes(s), :]))
 
+        keep_busy(5)
         h_banks0 = transposed_h(0)
+        keep_busy(3)
         bias_bank = psum_turns.tile([P, HALF], F32, tag="turn")
         nc.tensor.transpose(bias_bank[:, 0:P], bias_rows[:].bitcast(F32), ident[:])
         gate_bias = const.tile([P, GATES * LANES], F32)
+        keep_busy(4)
         h_lanes0 = h_in_sbuf(0, h_banks0)
-        group_u(Z, 0, nc.vector.tensor_copy)
+        for u in range(BLOCKS):
+            group_u(Z, u, nc.vector.tensor_copy)
+        nc.vector.tensor_copy(out=gate_bias[:], in_=bias_bank[:, 0 : GATES * BLOCKS].bitcast(BF16))
         h_mx0 = quantise_h(0, h_lanes0)
         quantise_u(Z, 0, CHANNELS // 2)
-        group_u(Z, 1, nc.vector.tensor_copy)
-        nc.vector.tensor_copy(out=gate_bias[:], in_=bias_bank[:, 0 : GATES * BLOCKS].bitcast(BF16))
         quantise_u(Z, CHANNELS // 2, CHANNELS // 2)
         x_words = words_in_sbuf(0, Z, transposed_gx_blocks(0, Z))
         group_u(R, 0, nc.scalar.copy)
@@ -381,10 +394,12 @@ def tile_gatedgraphconvolution_pb_kernel(
             add_gate_sum(z_sums[0], Z, t, gh, x_words)
             if t == LANES - 2:
                 quantise_u(R)
+        keep_busy(2)
         x_words = words_in_sbuf(0, R, transposed_gx_blocks(0, R))
-        for u in range(BLOCKS):
-            group_u(CAND, u, gpsimd_copy)
+        group_u(CAND, 0, nc.scalar.copy)
+        group_u(CAND, 1, gpsimd_copy)
 
+        keep_busy(2)
         gh = gh_banks(h_mx0, R)
         for t in range(LANES):
             if t == LANES - 1:
@@ -395,6 +410,7 @@ def tile_gatedgraphconvolution_pb_kernel(
                 keep_on_gpsimd(kept[0], z[0], h_lanes0, 0)
             sigmoid_r(r_sums[0], t)
 
+        keep_busy(3)
         h_lanes1 = h_in_sbuf(1, transposed_h(1))
         paired_function(z[0], z_sums[0], 1, ACT.Sigmoid)
         keep_on_gpsimd(kept[0], z[0], h_lanes0, 1)
@@ -410,6 +426,7 @@ def tile_gatedgraphconvolution_pb_kernel(
         for u in range(BLOCKS):
             paired_function(cand[0], products, u, ACT.Tanh)
 
+        keep_busy(3)
         gh = gh_banks(h_mx1, Z)
         for t in range(LANES):
             add_gate_sum(z_sums[1], Z, t, gh, x_words)
@@ -423,12 +440,17 @@ def tile_gatedgraphconvolution_pb_kernel(
             new_state(nc.gpsimd, hnew[0], kept[0], cand[0], slice(a * P, (a + 1) * P))
         keep_on_gpsimd(kept[1], z[1], h_lanes1, 0)
 
-        gh = gh_banks(h_mx1, R)
+        group_w()
+
+        keep_busy(3)
+        gh = [gh_bank(h_mx1, R, 0)]
+        keep_busy(4)
+        for t in range(1, LANES):
+            gh.append(gh_bank(h_mx1, R, t))
         for t in range(LANES):
             add_gate_sum(r_sums[1], R, t, gh, x_words)
             sigmoid_r(r_sums[1], t)
         paired_function(z[1], z_sums[1], 1, ACT.Sigmoid)
-        group_w()
 
         x_banks = transposed_gx_blocks(1, CAND)
         gh = gh_banks(h_mx1, CAND)

@@ -122,6 +122,8 @@ def tile_gatedgraphconvolution_pb_kernel(
 
         ident = const.tile([P, P], F32)
         make_identity(nc, ident[:])
+        ident_bf16 = const.tile([P, P], BF16)
+        make_identity(nc, ident_bf16[:])
 
         nc.scalar.activation(out=warm[:], in_=zeros[:, 0:1], func=ACT.Sigmoid)
 
@@ -242,6 +244,18 @@ def tile_gatedgraphconvolution_pb_kernel(
 
         idle_bank = psum_idle.tile([P, HALF], F32)
 
+        def keep_busy_mx(count):
+            for i in range(count):
+                nc.tensor.matmul_mx(
+                    out=idle_bank[:],
+                    lhsT=u_codes[Z][:, 0:P].bitcast(FP8X4),
+                    lhsT_scale=u_scales[Z][:, 0:P],
+                    rhs=h_mx0[0][:].bitcast(FP8X4),
+                    rhs_scale=h_mx0[1][:],
+                    start=True,
+                    stop=True,
+                )
+
         def keep_busy(count):
             for i in range(count):
                 nc.tensor.matmul(
@@ -261,10 +275,10 @@ def tile_gatedgraphconvolution_pb_kernel(
                 op1=ALU.add,
             )
 
-        def paired_function(out, lanes, u, func):
+        def paired_function(out, lanes, u, nodes, func):
             nc.scalar.activation(
-                out=out[:, u, :, :],
-                in_=lanes[:, lanes_of_block(u), :].rearrange("q e n -> q n e"),
+                out=out[:, u, nodes, :],
+                in_=lanes[:, lanes_of_block(u), nodes].rearrange("q e n -> q n e"),
                 func=func,
             )
 
@@ -291,20 +305,52 @@ def tile_gatedgraphconvolution_pb_kernel(
                 op1=ALU.mult,
             )
 
-        def candidate_sum(products, t, x_bank):
+        def transposed_gx_slice(half, gate, s):
+            bank = psum_turns.tile([P, BLOCKS, SLICE], F32, tag="turn")
+            for u in range(BLOCKS):
+                for j in range(READ_TILES):
+                    nc.tensor.transpose(
+                        bank[:, u, j * P : (j + 1) * P],
+                        gx_sb[half][gate][:, s * READ_TILES + j, :].bitcast(F32)[:, u * P : (u + 1) * P],
+                        ident[:],
+                    )
+            return bank
+
+        def candidate_sum_on_vector(products, t, x_bank, s):
             nc.vector.tensor_tensor(
-                out=products[:, t, :],
-                in0=products[:, t, :],
-                in1=lane_of_words(x_bank[:], t % PAIR),
+                out=products[:, t, slice_nodes(s)],
+                in0=products[:, t, slice_nodes(s)],
+                in1=lane_of_words(x_bank[:, t // PAIR, :], t % PAIR),
                 op=ALU.add,
             )
 
-        def minus_new(cand, z, u):
+        def candidate_sum_on_tensor(half, a, products):
+            bank = psum_turns.tile([P, LANES, P], F32, tag="turn")
+            for t in range(LANES):
+                first = PAIR * P * (t // PAIR) + t % PAIR
+                nc.tensor.matmul(
+                    out=bank[:, t, :],
+                    lhsT=gx_sb[half][CAND][:, a, first : first + PAIR * P - 1 : PAIR],
+                    rhs=ident_bf16[:],
+                    start=True,
+                    stop=False,
+                )
+                nc.tensor.matmul(
+                    out=bank[:, t, :],
+                    lhsT=ident[:],
+                    rhs=products[:, t, a * P : (a + 1) * P],
+                    start=False,
+                    stop=True,
+                )
+            return bank
+
+
+        def minus_new(cand, z, nodes):
             nc.vector.scalar_tensor_tensor(
-                out=cand[:, u, :, :],
-                in0=z[:, u, :, :],
+                out=cand[:, :, nodes, :],
+                in0=z[:, :, nodes, :],
                 scalar=1.0,
-                in1=cand[:, u, :, :],
+                in1=cand[:, :, nodes, :],
                 op0=ALU.subtract,
                 op1=ALU.mult,
             )
@@ -343,16 +389,18 @@ def tile_gatedgraphconvolution_pb_kernel(
                 )
             return bank
 
-        def store_result(half, s, bank):
-            result = work.tile([P, READ_TILES, OUTPUTS], F32, tag="result")
-            nc.vector.tensor_tensor(
-                out=result[:],
-                in0=bank[:],
-                in1=dense_bias[:].unsqueeze(1).to_broadcast([P, READ_TILES, OUTPUTS]),
-                op=ALU.add,
-            )
-            first_tile = half * HALF_TILES + s * READ_TILES
-            nc.sync.dma_start(out=out_rows[:, first_tile : first_tile + READ_TILES, :], in_=result[:])
+        def store_result(half, s, bank, pieces=1):
+            tiles = READ_TILES // pieces
+            for piece in range(pieces):
+                result = halves.tile([P, tiles, OUTPUTS], F32, name="result%d_%d_%d" % (half, s, piece))
+                nc.vector.tensor_tensor(
+                    out=result[:],
+                    in0=bank[:, piece * tiles : (piece + 1) * tiles, :],
+                    in1=dense_bias[:].unsqueeze(1).to_broadcast([P, tiles, OUTPUTS]),
+                    op=ALU.add,
+                )
+                first_tile = half * HALF_TILES + s * READ_TILES + piece * tiles
+                nc.sync.dma_start(out=out_rows[:, first_tile : first_tile + tiles, :], in_=result[:])
 
         z = []
         z_sums = []
@@ -367,6 +415,17 @@ def tile_gatedgraphconvolution_pb_kernel(
             kept.append(halves.tile([P, BLOCKS, HALF, PAIR], F32, name="kept%d" % half))
             hnew.append(halves.tile([P, HALF, LANES], BF16, name="hnew%d" % half, align_bytes=64))
             cand.append(halves.tile([P, BLOCKS, HALF, PAIR], F32, name="cand%d" % half))
+
+        all_nodes = slice(0, HALF)
+
+        def candidate_tiles(half, products, tiles):
+            for a in tiles:
+                sums = candidate_sum_on_tensor(half, a, products)
+                nc.scalar.activation(
+                    out=cand[half][:, :, a * P : (a + 1) * P, :],
+                    in_=sums[:].rearrange("q (u e) n -> q u n e", u=BLOCKS),
+                    func=ACT.Tanh,
+                )
 
         def read_out(half, s):
             return readout(quantise_new_state(hnew[half][:, slice_nodes(s), :]))
@@ -394,27 +453,28 @@ def tile_gatedgraphconvolution_pb_kernel(
             add_gate_sum(z_sums[0], Z, t, gh, x_words)
             if t == LANES - 2:
                 quantise_u(R)
-        keep_busy(2)
+        keep_busy_mx(2)
         x_words = words_in_sbuf(0, R, transposed_gx_blocks(0, R))
         group_u(CAND, 0, nc.scalar.copy)
         group_u(CAND, 1, gpsimd_copy)
 
-        keep_busy(2)
+        keep_busy_mx(2)
         gh = gh_banks(h_mx0, R)
         for t in range(LANES):
             if t == LANES - 1:
                 quantise_u(CAND)
             add_gate_sum(r_sums[0], R, t, gh, x_words)
             if t == 1:
-                paired_function(z[0], z_sums[0], 0, ACT.Sigmoid)
+                paired_function(z[0], z_sums[0], 0, all_nodes, ACT.Sigmoid)
                 keep_on_gpsimd(kept[0], z[0], h_lanes0, 0)
             sigmoid_r(r_sums[0], t)
 
-        keep_busy(3)
+        keep_busy_mx(2)
         h_lanes1 = h_in_sbuf(1, transposed_h(1))
-        paired_function(z[0], z_sums[0], 1, ACT.Sigmoid)
+        paired_function(z[0], z_sums[0], 1, all_nodes, ACT.Sigmoid)
         keep_on_gpsimd(kept[0], z[0], h_lanes0, 1)
-        x_banks = transposed_gx_blocks(0, CAND)
+        keep_busy_mx(1)
+        x_bank = transposed_gx_slice(0, CAND, 0)
         gh = gh_banks(h_mx0, CAND)
         products = halves.tile([P, LANES, HALF], F32, name="products0")
         for t in range(LANES):
@@ -422,19 +482,22 @@ def tile_gatedgraphconvolution_pb_kernel(
         h_mx1 = quantise_h(1, h_lanes1)
         x_words = words_in_sbuf(1, Z, transposed_gx_blocks(1, Z))
         for t in range(LANES):
-            candidate_sum(products, t, x_banks[t // PAIR])
+            candidate_sum_on_vector(products, t, x_bank, 0)
         for u in range(BLOCKS):
-            paired_function(cand[0], products, u, ACT.Tanh)
+            paired_function(cand[0], products, u, slice_nodes(0), ACT.Tanh)
+        candidate_tiles(0, products, (2,))
 
-        keep_busy(3)
-        gh = gh_banks(h_mx1, Z)
+        gh = []
+        for t in range(3):
+            gh.append(gh_bank(h_mx1, Z, t))
+        candidate_tiles(0, products, (3,))
+        gh.append(gh_bank(h_mx1, Z, 3))
         for t in range(LANES):
             add_gate_sum(z_sums[1], Z, t, gh, x_words)
-            if t == 1:
-                for u in range(BLOCKS):
-                    minus_new(cand[0], z[0], u)
+            if t % PAIR == 1:
+                minus_new(cand[0], z[0], slice_nodes(t // PAIR))
         x_words = words_in_sbuf(1, R, transposed_gx_blocks(1, R))
-        paired_function(z[1], z_sums[1], 0, ACT.Sigmoid)
+        paired_function(z[1], z_sums[1], 0, all_nodes, ACT.Sigmoid)
 
         for a in range(HALF_TILES):
             new_state(nc.gpsimd, hnew[0], kept[0], cand[0], slice(a * P, (a + 1) * P))
@@ -442,38 +505,35 @@ def tile_gatedgraphconvolution_pb_kernel(
 
         group_w()
 
-        keep_busy(3)
-        gh = [gh_bank(h_mx1, R, 0)]
-        keep_busy(4)
-        for t in range(1, LANES):
-            gh.append(gh_bank(h_mx1, R, t))
+        gh = gh_banks(h_mx1, R)
         for t in range(LANES):
             add_gate_sum(r_sums[1], R, t, gh, x_words)
             sigmoid_r(r_sums[1], t)
-        paired_function(z[1], z_sums[1], 1, ACT.Sigmoid)
+        paired_function(z[1], z_sums[1], 1, all_nodes, ACT.Sigmoid)
 
-        x_banks = transposed_gx_blocks(1, CAND)
+        x_bank = transposed_gx_slice(1, CAND, 0)
         gh = gh_banks(h_mx1, CAND)
         products = halves.tile([P, LANES, HALF], F32, name="products1")
         for t in range(LANES):
             reset_product(products, t, gh, r_sums[1])
         for t in range(LANES):
-            candidate_sum(products, t, x_banks[t // PAIR])
+            candidate_sum_on_vector(products, t, x_bank, 0)
         for u in range(BLOCKS):
-            paired_function(cand[1], products, u, ACT.Tanh)
+            paired_function(cand[1], products, u, slice_nodes(0), ACT.Tanh)
+        candidate_tiles(1, products, (2, 3))
 
         keep_state(nc.vector, kept[1], z[1], h_lanes1, 1, slice(0, HALF))
         quantise_w()
         banks0 = []
         for s in range(SLICES):
             banks0.append(read_out(0, s))
-        minus_new(cand[1], z[1], 0)
+        minus_new(cand[1], z[1], slice_nodes(0))
         store_result(0, 0, banks0[0])
-        minus_new(cand[1], z[1], 1)
-        store_result(0, 1, banks0[1])
         new_state(nc.vector, hnew[1], kept[1], cand[1], slice_nodes(0))
-        new_state(nc.vector, hnew[1], kept[1], cand[1], slice_nodes(1))
+        minus_new(cand[1], z[1], slice_nodes(1))
         bank = read_out(1, 0)
-        bank_last = read_out(1, 1)
+        new_state(nc.vector, hnew[1], kept[1], cand[1], slice_nodes(1))
+        store_result(0, 1, banks0[1])
+        last_bank = read_out(1, 1)
         store_result(1, 0, bank)
-        store_result(1, 1, bank_last)
+        store_result(1, 1, last_bank, pieces=READ_TILES)

@@ -438,8 +438,8 @@ def tile_gatedgraphconvolution_pb_kernel(
         gate_bias = const.tile([P, GATES * LANES], F32)
         keep_busy(4)
         h_lanes0 = h_in_sbuf(0, h_banks0)
-        for u in range(BLOCKS):
-            group_u(Z, u, nc.vector.tensor_copy)
+        group_u(Z, 0, nc.vector.tensor_copy)
+        group_u(Z, 1, nc.scalar.copy)
         nc.vector.tensor_copy(out=gate_bias[:], in_=bias_bank[:, 0 : GATES * BLOCKS].bitcast(BF16))
         h_mx0 = quantise_h(0, h_lanes0)
         quantise_u(Z, 0, CHANNELS // 2)
@@ -501,7 +501,7 @@ def tile_gatedgraphconvolution_pb_kernel(
 
         for a in range(HALF_TILES):
             new_state(nc.gpsimd, hnew[0], kept[0], cand[0], slice(a * P, (a + 1) * P))
-        keep_on_gpsimd(kept[1], z[1], h_lanes1, 0)
+        keep_state(nc.gpsimd, kept[1], z[1], h_lanes1, 0, slice_nodes(0))
 
         group_w()
 
@@ -523,6 +523,7 @@ def tile_gatedgraphconvolution_pb_kernel(
         candidate_tiles(1, products, (2, 3))
 
         keep_state(nc.vector, kept[1], z[1], h_lanes1, 1, slice(0, HALF))
+        keep_state(nc.vector, kept[1], z[1], h_lanes1, 0, slice_nodes(1))
         quantise_w()
         banks0 = []
         for s in range(SLICES):

@@ -430,9 +430,9 @@ def tile_gatedgraphconvolution_pb_kernel(
         def read_out(half, s):
             return readout(quantise_new_state(hnew[half][:, slice_nodes(s), :]))
 
-        keep_busy(5)
+        keep_busy(6)
         h_banks0 = transposed_h(0)
-        keep_busy(3)
+        keep_busy(2)
         bias_bank = psum_turns.tile([P, HALF], F32, tag="turn")
         nc.tensor.transpose(bias_bank[:, 0:P], bias_rows[:].bitcast(F32), ident[:])
         gate_bias = const.tile([P, GATES * LANES], F32)
@@ -453,12 +453,12 @@ def tile_gatedgraphconvolution_pb_kernel(
             add_gate_sum(z_sums[0], Z, t, gh, x_words)
             if t == LANES - 2:
                 quantise_u(R)
-        keep_busy_mx(2)
+        keep_busy_mx(3)
         x_words = words_in_sbuf(0, R, transposed_gx_blocks(0, R))
         group_u(CAND, 0, nc.scalar.copy)
         group_u(CAND, 1, gpsimd_copy)
 
-        keep_busy_mx(2)
+        keep_busy_mx(3)
         gh = gh_banks(h_mx0, R)
         for t in range(LANES):
             if t == LANES - 1:
@@ -469,17 +469,20 @@ def tile_gatedgraphconvolution_pb_kernel(
                 keep_on_gpsimd(kept[0], z[0], h_lanes0, 0)
             sigmoid_r(r_sums[0], t)
 
-        keep_busy_mx(2)
+        keep_busy_mx(4)
         h_lanes1 = h_in_sbuf(1, transposed_h(1))
         paired_function(z[0], z_sums[0], 1, all_nodes, ACT.Sigmoid)
         keep_on_gpsimd(kept[0], z[0], h_lanes0, 1)
-        keep_busy_mx(1)
+        gh = []
+        for t in range(LANES - 1):
+            gh.append(gh_bank(h_mx0, CAND, t))
         x_bank = transposed_gx_slice(0, CAND, 0)
-        gh = gh_banks(h_mx0, CAND)
+        gh.append(gh_bank(h_mx0, CAND, LANES - 1))
         products = halves.tile([P, LANES, HALF], F32, name="products0")
         for t in range(LANES):
             reset_product(products, t, gh, r_sums[0])
         h_mx1 = quantise_h(1, h_lanes1)
+        keep_busy_mx(1)
         x_words = words_in_sbuf(1, Z, transposed_gx_blocks(1, Z))
         for t in range(LANES):
             candidate_sum_on_vector(products, t, x_bank, 0)

@@ -324,26 +324,28 @@ def tile_gatedgraphconvolution_pb_kernel(
                 op=ALU.add,
             )
 
-        def candidate_sum_on_tensor(half, a, products):
-            bank = psum_turns.tile([P, LANES, P], F32, tag="turn")
-            for t in range(LANES):
-                first = PAIR * P * (t // PAIR) + t % PAIR
+        def candidate_sum_on_tensor(half, u, s, products):
+            bank = psum_turns.tile([P, PAIR, SLICE], F32, tag="turn")
+            for e in range(PAIR):
+                for j in range(READ_TILES):
+                    first = PAIR * P * u + e
+                    nc.tensor.matmul(
+                        out=bank[:, e, j * P : (j + 1) * P],
+                        lhsT=gx_sb[half][CAND][
+                            :, s * READ_TILES + j, first : first + PAIR * P - 1 : PAIR
+                        ],
+                        rhs=ident_bf16[:],
+                        start=(j == 0),
+                        stop=False,
+                    )
                 nc.tensor.matmul(
-                    out=bank[:, t, :],
-                    lhsT=gx_sb[half][CAND][:, a, first : first + PAIR * P - 1 : PAIR],
-                    rhs=ident_bf16[:],
-                    start=True,
-                    stop=False,
-                )
-                nc.tensor.matmul(
-                    out=bank[:, t, :],
+                    out=bank[:, e, :],
                     lhsT=ident[:],
-                    rhs=products[:, t, a * P : (a + 1) * P],
+                    rhs=products[:, PAIR * u + e, slice_nodes(s)],
                     start=False,
                     stop=True,
                 )
             return bank
-
 
         def minus_new(cand, z, nodes):
             nc.vector.scalar_tensor_tensor(
@@ -418,25 +420,24 @@ def tile_gatedgraphconvolution_pb_kernel(
 
         all_nodes = slice(0, HALF)
 
-        def candidate_tiles(half, products, tiles):
-            for a in tiles:
-                sums = candidate_sum_on_tensor(half, a, products)
-                nc.scalar.activation(
-                    out=cand[half][:, :, a * P : (a + 1) * P, :],
-                    in_=sums[:].rearrange("q (u e) n -> q u n e", u=BLOCKS),
-                    func=ACT.Tanh,
-                )
+        def candidate_block(half, products, u, s):
+            sums = candidate_sum_on_tensor(half, u, s, products)
+            nc.scalar.activation(
+                out=cand[half][:, u, slice_nodes(s), :],
+                in_=sums[:].rearrange("q e n -> q n e"),
+                func=ACT.Tanh,
+            )
 
         def read_out(half, s):
             return readout(quantise_new_state(hnew[half][:, slice_nodes(s), :]))
 
-        keep_busy(6)
+        keep_busy(5)
         h_banks0 = transposed_h(0)
         keep_busy(2)
         bias_bank = psum_turns.tile([P, HALF], F32, tag="turn")
         nc.tensor.transpose(bias_bank[:, 0:P], bias_rows[:].bitcast(F32), ident[:])
         gate_bias = const.tile([P, GATES * LANES], F32)
-        keep_busy(4)
+        keep_busy(3)
         h_lanes0 = h_in_sbuf(0, h_banks0)
         group_u(Z, 0, nc.vector.tensor_copy)
         group_u(Z, 1, nc.scalar.copy)
@@ -453,12 +454,12 @@ def tile_gatedgraphconvolution_pb_kernel(
             add_gate_sum(z_sums[0], Z, t, gh, x_words)
             if t == LANES - 2:
                 quantise_u(R)
-        keep_busy_mx(3)
+        keep_busy_mx(1)
         x_words = words_in_sbuf(0, R, transposed_gx_blocks(0, R))
         group_u(CAND, 0, nc.scalar.copy)
         group_u(CAND, 1, gpsimd_copy)
 
-        keep_busy_mx(3)
+        keep_busy_mx(1)
         gh = gh_banks(h_mx0, R)
         for t in range(LANES):
             if t == LANES - 1:
@@ -469,7 +470,7 @@ def tile_gatedgraphconvolution_pb_kernel(
                 keep_on_gpsimd(kept[0], z[0], h_lanes0, 0)
             sigmoid_r(r_sums[0], t)
 
-        keep_busy_mx(4)
+        keep_busy_mx(3)
         h_lanes1 = h_in_sbuf(1, transposed_h(1))
         paired_function(z[0], z_sums[0], 1, all_nodes, ACT.Sigmoid)
         keep_on_gpsimd(kept[0], z[0], h_lanes0, 1)
@@ -488,12 +489,12 @@ def tile_gatedgraphconvolution_pb_kernel(
             candidate_sum_on_vector(products, t, x_bank, 0)
         for u in range(BLOCKS):
             paired_function(cand[0], products, u, slice_nodes(0), ACT.Tanh)
-        candidate_tiles(0, products, (2,))
+        candidate_block(0, products, 0, 1)
 
         gh = []
         for t in range(3):
             gh.append(gh_bank(h_mx1, Z, t))
-        candidate_tiles(0, products, (3,))
+        candidate_block(0, products, 1, 1)
         gh.append(gh_bank(h_mx1, Z, 3))
         for t in range(LANES):
             add_gate_sum(z_sums[1], Z, t, gh, x_words)
@@ -504,7 +505,7 @@ def tile_gatedgraphconvolution_pb_kernel(
 
         for a in range(HALF_TILES):
             new_state(nc.gpsimd, hnew[0], kept[0], cand[0], slice(a * P, (a + 1) * P))
-        keep_state(nc.gpsimd, kept[1], z[1], h_lanes1, 0, slice_nodes(0))
+        keep_on_gpsimd(kept[1], z[1], h_lanes1, 0)
 
         group_w()
 
@@ -523,10 +524,10 @@ def tile_gatedgraphconvolution_pb_kernel(
             candidate_sum_on_vector(products, t, x_bank, 0)
         for u in range(BLOCKS):
             paired_function(cand[1], products, u, slice_nodes(0), ACT.Tanh)
-        candidate_tiles(1, products, (2, 3))
+        for u in range(BLOCKS):
+            candidate_block(1, products, u, 1)
 
         keep_state(nc.vector, kept[1], z[1], h_lanes1, 1, slice(0, HALF))
-        keep_state(nc.vector, kept[1], z[1], h_lanes1, 0, slice_nodes(1))
         quantise_w()
         banks0 = []
         for s in range(SLICES):

from contextlib import ExitStack

import concourse.mybir as mybir
from concourse.masks import make_identity

FP8X4 = mybir.dt.float8_e4m3fn_x4
BF16 = mybir.dt.bfloat16
F32 = mybir.dt.float32
U32 = mybir.dt.uint32
U8 = mybir.dt.uint8
ALU = mybir.AluOpType
ACT = mybir.ActivationFunctionType

P = 128
LANES = 4
BLOCKS = 2
PAIR = 2
NODES = 1024
CHANNELS = 512
GATES = 3
Z = 0
R = 1
CAND = 2
OUTPUTS = 256
NODE_TILES = NODES // P
HALVES = 2
HALF_TILES = NODE_TILES // HALVES
HALF = HALF_TILES * P
READ_TILES = 2
SLICE = READ_TILES * P
SLICES = HALF // SLICE

FLOPS = 2 * NODES * CHANNELS * (GATES * CHANNELS + OUTPUTS)


def lane_of_words(words, e):
    return words.bitcast(BF16).rearrange("p (n e) -> p n e", e=PAIR)[:, :, e]


def lanes_of_block(u):
    return slice(PAIR * u, PAIR * (u + 1))


def slice_nodes(s):
    return slice(s * SLICE, (s + 1) * SLICE)


def tile_gatedgraphconvolution_pb_kernel(
    tc, gx, annotations, gru_U, gru_b_h, dense_W, dense_b, out
):
    nc = tc.nc
    h_rows = annotations.flatten_outer_dims().rearrange("(p a) c -> p a c", a=NODE_TILES)
    gx_rows = gx.rearrange("(p a) g -> p a g", a=NODE_TILES)
    out_rows = out.flatten_outer_dims().rearrange("(p a) o -> p a o", a=NODE_TILES)

    with ExitStack() as ctx:
        const = ctx.enter_context(tc.tile_pool(name="const", bufs=1))
        inputs = ctx.enter_context(tc.tile_pool(name="inputs", bufs=1))
        weights = ctx.enter_context(tc.tile_pool(name="weights", bufs=1))
        halves = ctx.enter_context(tc.tile_pool(name="halves", bufs=1))
        work = ctx.enter_context(tc.tile_pool(name="work", bufs=HALVES * SLICES))
        psum_gh = ctx.enter_context(tc.psum_pool(name="psum_gh", bufs=3))
        psum_turns = ctx.enter_context(tc.psum_pool(name="psum_turns", bufs=4))
        psum_idle = ctx.enter_context(tc.psum_pool(name="psum_idle", bufs=1))
        ctx.enter_context(tc.manual_schedule())

        h_sb = []
        gx_sb = []
        for half in range(HALVES):
            h_sb.append(inputs.tile([P, HALF_TILES, CHANNELS], BF16, name="h_sb%d" % half))
            gx_sb.append([])
            for gate in range(GATES):
                gx_sb[half].append(
                    inputs.tile([P, HALF_TILES, CHANNELS], BF16, name="gx_sb%d_%d" % (half, gate))
                )
        u_raw = []
        for gate in range(GATES):
            u_raw.append(weights.tile([P, LANES, CHANNELS], BF16, name="u_raw%d" % gate))
        w_raw = weights.tile([P, LANES, OUTPUTS], BF16)
        bias_rows = const.tile([P, PAIR * P], BF16)
        dense_bias = const.tile([P, OUTPUTS], BF16)

        def load_lanes(raw, rows):
            for u in range(BLOCKS):
                nc.sync.dma_start(
                    out=raw[:, lanes_of_block(u), :],
                    in_=rows[PAIR * P * u : PAIR * P * (u + 1), :].rearrange(
                        "(q e) w -> q e w", e=PAIR
                    ),
                )

        def load_u(gate):
            load_lanes(u_raw[gate], gru_U[:, gate * CHANNELS : (gate + 1) * CHANNELS])

        def load_h(half):
            tiles = slice(half * HALF_TILES, (half + 1) * HALF_TILES)
            nc.sync.dma_start(out=h_sb[half][:], in_=h_rows[:, tiles, :])

        def load_gx(half, gate):
            tiles = slice(half * HALF_TILES, (half + 1) * HALF_TILES)
            cols = slice(gate * CHANNELS, (gate + 1) * CHANNELS)
            nc.sync.dma_start(out=gx_sb[half][gate][:], in_=gx_rows[:, tiles, cols])

        zeros = const.tile([P, P], F32)
        warm = const.tile([P, 1], F32)
        nc.vector.memset(zeros[:], 0.0)
        load_h(0)
        load_u(Z)
        nc.vector.memset(bias_rows[:], 0.0)
        bias_source = gru_b_h.rearrange("(r c) -> r c", c=PAIR * P)
        for rows in (slice(0, 4), slice(4, 6)):
            nc.sync.dma_start(out=bias_rows[rows, :], in_=bias_source[rows, :])
        load_gx(0, Z)
        for gate in (R, CAND):
            load_u(gate)
            load_gx(0, gate)
        load_h(1)
        for gate in range(GATES):
            load_gx(1, gate)
        load_lanes(w_raw, dense_W)
        nc.sync.dma_start(out=dense_bias[:], in_=dense_b.partition_broadcast(P))

        ident = const.tile([P, P], F32)
        make_identity(nc, ident[:])
        ident_bf16 = const.tile([P, P], BF16)
        make_identity(nc, ident_bf16[:])

        nc.scalar.activation(out=warm[:], in_=zeros[:, 0:1], func=ACT.Sigmoid)

        u_grouped = []
        u_codes = []
        u_scales = []
        for gate in range(GATES):
            u_grouped.append(
                weights.tile([P, CHANNELS, LANES], BF16, name="u_grouped%d" % gate, align_bytes=64)
            )
            u_codes.append(weights.tile([P, CHANNELS], U32, name="u_codes%d" % gate, align_bytes=64))
            u_scales.append(weights.tile([P, CHANNELS], U8, name="u_scales%d" % gate, align_bytes=64))
        w_grouped = weights.tile([P, OUTPUTS, LANES], BF16, align_bytes=64)
        w_codes = weights.tile([P, OUTPUTS], U32, align_bytes=64)
        w_scales = weights.tile([P, OUTPUTS], U8, align_bytes=64)

        def gpsimd_copy(out, in_):
            nc.gpsimd.tensor_scalar(
                out=out, in0=in_, scalar1=1.0, scalar2=0.0, op0=ALU.mult, op1=ALU.add
            )

        def group_u(gate, u, copy):
            block = slice(PAIR * P * u, PAIR * P * (u + 1))
            copy(
                out=u_grouped[gate][:, block, :].rearrange("k (e q) t -> k e q t", e=PAIR),
                in_=u_raw[gate][:, :, block].rearrange("k t (q e) -> k e q t", e=PAIR),
            )

        def quantise_u(gate, first=0, count=CHANNELS):
            positions = slice(first, first + count)
            nc.vector.quantize_mx(
                out=u_codes[gate][:, positions].bitcast(FP8X4),
                scales=u_scales[gate][:, positions],
                in_=u_grouped[gate][:, positions, :].rearrange("k w t -> k (w t)"),
            )

        def group_w():
            nc.scalar.copy(out=w_grouped[:], in_=w_raw[:].rearrange("k t w -> k w t"))

        def quantise_w():
            nc.vector.quantize_mx(
                out=w_codes[:].bitcast(FP8X4),
                scales=w_scales[:],
                in_=w_grouped[:].rearrange("k w t -> k (w t)"),
            )

        def transposed_gx(half, gate, u):
            bank = psum_turns.tile([P, HALF], F32, tag="turn")
            for a in range(HALF_TILES):
                nc.tensor.transpose(
                    bank[:, a * P : (a + 1) * P],
                    gx_sb[half][gate][:, a, :].bitcast(F32)[:, u * P : (u + 1) * P],
                    ident[:],
                )
            return bank

        def transposed_gx_blocks(half, gate):
            banks = []
            for u in range(BLOCKS):
                banks.append(transposed_gx(half, gate, u))
            return banks

        def words_in_sbuf(half, gate, banks):
            x_words = halves.tile([P, BLOCKS, HALF], F32, name="x_words%d_%d" % (half, gate))
            for u in range(BLOCKS):
                nc.scalar.copy(out=x_words[:, u, :], in_=banks[u][:])
            return x_words

        def transposed_h(half):
            banks = []
            for s in range(HALF_TILES // PAIR):
                bank = psum_turns.tile([P, BLOCKS, PAIR * P], F32, tag="turn")
                for u in range(BLOCKS):
                    for j in range(PAIR):
                        nc.tensor.transpose(
                            bank[:, u, j * P : (j + 1) * P],
                            h_sb[half][:, PAIR * s + j, :].bitcast(F32)[:, u * P : (u + 1) * P],
                            ident[:],
                        )
                banks.append(bank)
            return banks

        def h_in_sbuf(half, banks):
            h_words = halves.tile([P, HALF, BLOCKS], F32, name="h_words%d" % half, align_bytes=64)
            for s in range(HALF_TILES // PAIR):
                nc.scalar.copy(
                    out=h_words[:, s * PAIR * P : (s + 1) * PAIR * P, :],
                    in_=banks[s][:].rearrange("q u n -> q n u"),
                )
            return h_words[:].rearrange("q n u -> q (n u)").bitcast(BF16)

        def quantise_h(half, h_lanes):
            h_codes = halves.tile([P, HALF], U32, name="h_codes%d" % half, align_bytes=64)
            h_scales = halves.tile([P, HALF], U8, name="h_scales%d" % half, align_bytes=64)
            nc.vector.quantize_mx(out=h_codes[:].bitcast(FP8X4), scales=h_scales[:], in_=h_lanes)
            return h_codes, h_scales

        def gh_bank(h_mx, gate, t):
            h_codes, h_scales = h_mx
            bank = psum_gh.tile([P, HALF], F32, tag="gh")
            positions = slice(t * P, (t + 1) * P)
            nc.tensor.matmul_mx(
                out=bank[:],
                lhsT=u_codes[gate][:, positions].bitcast(FP8X4),
                lhsT_scale=u_scales[gate][:, positions],
                rhs=h_codes[:].bitcast(FP8X4),
                rhs_scale=h_scales[:],
                start=True,
                stop=True,
            )
            return bank

        def gh_banks(h_mx, gate):
            banks = []
            for t in range(LANES):
                banks.append(gh_bank(h_mx, gate, t))
            return banks

        idle_bank = psum_idle.tile([P, HALF], F32)

        def keep_busy_mx(count):
            for i in range(count):
                nc.tensor.matmul_mx(
                    out=idle_bank[:],
                    lhsT=u_codes[Z][:, 0:P].bitcast(FP8X4),
                    lhsT_scale=u_scales[Z][:, 0:P],
                    rhs=h_mx0[0][:].bitcast(FP8X4),
                    rhs_scale=h_mx0[1][:],
                    start=True,
                    stop=True,
                )

        def keep_busy(count):
            for i in range(count):
                nc.tensor.matmul(
                    out=idle_bank[:, 0:P], lhsT=zeros[:], rhs=zeros[:], start=True, stop=True
                )

        def bias_of(gate, t):
            return gate_bias[:, gate * LANES + t : gate * LANES + t + 1]

        def add_gate_sum(sums, gate, t, gh, x_words):
            nc.vector.scalar_tensor_tensor(
                out=sums[:, t, :],
                in0=gh[t][:],
                scalar=bias_of(gate, t),
                in1=lane_of_words(x_words[:, t // PAIR, :], t % PAIR),
                op0=ALU.add,
                op1=ALU.add,
            )

        def paired_function(out, lanes, u, nodes, func):
            nc.scalar.activation(
                out=out[:, u, nodes, :],
                in_=lanes[:, lanes_of_block(u), nodes].rearrange("q e n -> q n e"),
                func=func,
            )

        def sigmoid_r(sums, t):
            nc.scalar.activation(out=sums[:, t, :], in_=sums[:, t, :], func=ACT.Sigmoid)

        def keep_state(engine, kept, z, h_lanes, u, nodes):
            h_pairs = h_lanes.rearrange("q (n u e) -> q u n e", u=BLOCKS, e=PAIR)
            engine.tensor_tensor(
                out=kept[:, u, nodes, :], in0=z[:, u, nodes, :], in1=h_pairs[:, u, nodes, :], op=ALU.mult
            )

        def keep_on_gpsimd(kept, z, h_lanes, u):
            for s in range(SLICES):
                keep_state(nc.gpsimd, kept, z, h_lanes, u, slice_nodes(s))

        def reset_product(products, t, gh, r):
            nc.vector.scalar_tensor_tensor(
                out=products[:, t, :],
                in0=gh[t][:],
                scalar=bias_of(CAND, t),
                in1=r[:, t, :],
                op0=ALU.add,
                op1=ALU.mult,
            )

        def transposed_gx_slice(half, gate, s):
            bank = psum_turns.tile([P, BLOCKS, SLICE], F32, tag="turn")
            for u in range(BLOCKS):
                for j in range(READ_TILES):
                    nc.tensor.transpose(
                        bank[:, u, j * P : (j + 1) * P],
                        gx_sb[half][gate][:, s * READ_TILES + j, :].bitcast(F32)[:, u * P : (u + 1) * P],
                        ident[:],
                    )
            return bank

        def candidate_sum_on_vector(products, t, x_bank, s):
            nc.vector.tensor_tensor(
                out=products[:, t, slice_nodes(s)],
                in0=products[:, t, slice_nodes(s)],
                in1=lane_of_words(x_bank[:, t // PAIR, :], t % PAIR),
                op=ALU.add,
            )

        def candidate_sum_on_tensor(half, u, s, products):
            bank = psum_turns.tile([P, PAIR, SLICE], F32, tag="turn")
            for e in range(PAIR):
                for j in range(READ_TILES):
                    first = PAIR * P * u + e
                    nc.tensor.matmul(
                        out=bank[:, e, j * P : (j + 1) * P],
                        lhsT=gx_sb[half][CAND][
                            :, s * READ_TILES + j, first : first + PAIR * P - 1 : PAIR
                        ],
                        rhs=ident_bf16[:],
                        start=(j == 0),
                        stop=False,
                    )
                nc.tensor.matmul(
                    out=bank[:, e, :],
                    lhsT=ident[:],
                    rhs=products[:, PAIR * u + e, slice_nodes(s)],
                    start=False,
                    stop=True,
                )
            return bank

        def minus_new(cand, z, nodes):
            nc.vector.scalar_tensor_tensor(
                out=cand[:, :, nodes, :],
                in0=z[:, :, nodes, :],
                scalar=1.0,
                in1=cand[:, :, nodes, :],
                op0=ALU.subtract,
                op1=ALU.mult,
            )

        def new_state(engine, hnew, kept, product, nodes):
            engine.tensor_tensor(
                out=hnew[:, nodes, :].rearrange("q n (u e) -> q n u e", u=BLOCKS),
                in0=kept[:, :, nodes, :].rearrange("q u n e -> q n u e"),
                in1=product[:, :, nodes, :].rearrange("q u n e -> q n u e"),
                op=ALU.subtract,
            )

        def quantise_new_state(hnew):
            codes = work.tile([P, SLICE], U32, tag="hnew_codes", align_bytes=64)
            scales = work.tile([P, SLICE], U8, tag="hnew_scales", align_bytes=64)
            nc.vector.quantize_mx(
                out=codes[:].bitcast(FP8X4),
                scales=scales[:],
                in_=hnew.rearrange("q n t -> q (n t)"),
            )
            return codes, scales

        def readout(hnew_mx):
            codes, scales = hnew_mx
            bank = psum_turns.tile([P, READ_TILES, OUTPUTS], F32, tag="turn")
            for j in range(READ_TILES):
                nodes = slice(j * P, (j + 1) * P)
                nc.tensor.matmul_mx(
                    out=bank[:, j, :],
                    lhsT=codes[:, nodes].bitcast(FP8X4),
                    lhsT_scale=scales[:, nodes],
                    rhs=w_codes[:].bitcast(FP8X4),
                    rhs_scale=w_scales[:],
                    start=True,
                    stop=True,
                )
            return bank

        def store_result(half, s, bank, pieces=1):
            tiles = READ_TILES // pieces
            for piece in range(pieces):
                result = halves.tile([P, tiles, OUTPUTS], F32, name="result%d_%d_%d" % (half, s, piece))
                nc.vector.tensor_tensor(
                    out=result[:],
                    in0=bank[:, piece * tiles : (piece + 1) * tiles, :],
                    in1=dense_bias[:].unsqueeze(1).to_broadcast([P, tiles, OUTPUTS]),
                    op=ALU.add,
                )
                first_tile = half * HALF_TILES + s * READ_TILES + piece * tiles
                nc.sync.dma_start(out=out_rows[:, first_tile : first_tile + tiles, :], in_=result[:])

        z = []
        z_sums = []
        r_sums = []
        kept = []
        hnew = []
        cand = []
        for half in range(HALVES):
            z.append(halves.tile([P, BLOCKS, HALF, PAIR], F32, name="z%d" % half))
            z_sums.append(halves.tile([P, LANES, HALF], F32, name="z_sums%d" % half))
            r_sums.append(halves.tile([P, LANES, HALF], F32, name="r_sums%d" % half))
            kept.append(halves.tile([P, BLOCKS, HALF, PAIR], F32, name="kept%d" % half))
            hnew.append(halves.tile([P, HALF, LANES], BF16, name="hnew%d" % half, align_bytes=64))
            cand.append(halves.tile([P, BLOCKS, HALF, PAIR], F32, name="cand%d" % half))

        all_nodes = slice(0, HALF)

        def candidate_block(half, products, u, s):
            sums = candidate_sum_on_tensor(half, u, s, products)
            nc.scalar.activation(
                out=cand[half][:, u, slice_nodes(s), :],
                in_=sums[:].rearrange("q e n -> q n e"),
                func=ACT.Tanh,
            )

        def read_out(half, s):
            return readout(quantise_new_state(hnew[half][:, slice_nodes(s), :]))

        keep_busy(5)
        h_banks0 = transposed_h(0)
        keep_busy(2)
        bias_bank = psum_turns.tile([P, HALF], F32, tag="turn")
        nc.tensor.transpose(bias_bank[:, 0:P], bias_rows[:].bitcast(F32), ident[:])
        gate_bias = const.tile([P, GATES * LANES], F32)
        keep_busy(3)
        h_lanes0 = h_in_sbuf(0, h_banks0)
        group_u(Z, 0, nc.vector.tensor_copy)
        group_u(Z, 1, nc.scalar.copy)
        nc.vector.tensor_copy(out=gate_bias[:], in_=bias_bank[:, 0 : GATES * BLOCKS].bitcast(BF16))
        h_mx0 = quantise_h(0, h_lanes0)
        quantise_u(Z, 0, CHANNELS // 2)
        quantise_u(Z, CHANNELS // 2, CHANNELS // 2)
        x_words = words_in_sbuf(0, Z, transposed_gx_blocks(0, Z))
        group_u(R, 0, nc.scalar.copy)
        group_u(R, 1, gpsimd_copy)

        gh = gh_banks(h_mx0, Z)
        for t in range(LANES):
            add_gate_sum(z_sums[0], Z, t, gh, x_words)
            if t == LANES - 2:
                quantise_u(R)
        keep_busy_mx(1)
        x_words = words_in_sbuf(0, R, transposed_gx_blocks(0, R))
        group_u(CAND, 0, nc.scalar.copy)
        group_u(CAND, 1, gpsimd_copy)

        keep_busy_mx(1)
        gh = gh_banks(h_mx0, R)
        for t in range(LANES):
            if t == LANES - 1:
                quantise_u(CAND)
            add_gate_sum(r_sums[0], R, t, gh, x_words)
            if t == 1:
                paired_function(z[0], z_sums[0], 0, all_nodes, ACT.Sigmoid)
                keep_on_gpsimd(kept[0], z[0], h_lanes0, 0)
            sigmoid_r(r_sums[0], t)

        keep_busy_mx(3)
        h_lanes1 = h_in_sbuf(1, transposed_h(1))
        paired_function(z[0], z_sums[0], 1, all_nodes, ACT.Sigmoid)
        keep_on_gpsimd(kept[0], z[0], h_lanes0, 1)
        gh = []
        for t in range(LANES - 1):
            gh.append(gh_bank(h_mx0, CAND, t))
        x_bank = transposed_gx_slice(0, CAND, 0)
        gh.append(gh_bank(h_mx0, CAND, LANES - 1))
        products = halves.tile([P, LANES, HALF], F32, name="products0")
        for t in range(LANES):
            reset_product(products, t, gh, r_sums[0])
        h_mx1 = quantise_h(1, h_lanes1)
        keep_busy_mx(1)
        x_words = words_in_sbuf(1, Z, transposed_gx_blocks(1, Z))
        for t in range(LANES):
            candidate_sum_on_vector(products, t, x_bank, 0)
        for u in range(BLOCKS):
            paired_function(cand[0], products, u, slice_nodes(0), ACT.Tanh)
        candidate_block(0, products, 0, 1)

        gh = []
        for t in range(3):
            gh.append(gh_bank(h_mx1, Z, t))
        candidate_block(0, products, 1, 1)
        gh.append(gh_bank(h_mx1, Z, 3))
        for t in range(LANES):
            add_gate_sum(z_sums[1], Z, t, gh, x_words)
            if t % PAIR == 1:
                minus_new(cand[0], z[0], slice_nodes(t // PAIR))
        x_words = words_in_sbuf(1, R, transposed_gx_blocks(1, R))
        paired_function(z[1], z_sums[1], 0, all_nodes, ACT.Sigmoid)

        for a in range(HALF_TILES):
            new_state(nc.gpsimd, hnew[0], kept[0], cand[0], slice(a * P, (a + 1) * P))
        keep_on_gpsimd(kept[1], z[1], h_lanes1, 0)

        group_w()

        gh = gh_banks(h_mx1, R)
        for t in range(LANES):
            add_gate_sum(r_sums[1], R, t, gh, x_words)
            sigmoid_r(r_sums[1], t)
        paired_function(z[1], z_sums[1], 1, all_nodes, ACT.Sigmoid)

        x_bank = transposed_gx_slice(1, CAND, 0)
        gh = gh_banks(h_mx1, CAND)
        products = halves.tile([P, LANES, HALF], F32, name="products1")
        for t in range(LANES):
            reset_product(products, t, gh, r_sums[1])
        for t in range(LANES):
            candidate_sum_on_vector(products, t, x_bank, 0)
        for u in range(BLOCKS):
            paired_function(cand[1], products, u, slice_nodes(0), ACT.Tanh)
        for u in range(BLOCKS):
            candidate_block(1, products, u, 1)

        keep_state(nc.vector, kept[1], z[1], h_lanes1, 1, slice(0, HALF))
        quantise_w()
        banks0 = []
        for s in range(SLICES):
            banks0.append(read_out(0, s))
        minus_new(cand[1], z[1], slice_nodes(0))
        store_result(0, 0, banks0[0])
        new_state(nc.vector, hnew[1], kept[1], cand[1], slice_nodes(0))
        minus_new(cand[1], z[1], slice_nodes(1))
        bank = read_out(1, 0)
        new_state(nc.vector, hnew[1], kept[1], cand[1], slice_nodes(1))
        store_result(0, 1, banks0[1])
        last_bank = read_out(1, 1)
        store_result(1, 0, bank)
        store_result(1, 1, last_bank, pieces=READ_TILES)
